import numpy as np
import ml_dtypes


def mxq(x, axis, fmt="e4m3"):
    dtype, down = {"e4m3": (ml_dtypes.float8_e4m3fn, 7), "e5m2": (ml_dtypes.float8_e5m2, 14)}[fmt]
    v = np.moveaxis(np.asarray(x, np.float32).astype(ml_dtypes.bfloat16).astype(np.float64), axis, -1)
    blocks = v.reshape(v.shape[:-1] + (-1, 32))
    amax = np.abs(blocks).max(-1, keepdims=True)
    byte = np.maximum(np.where(amax > 0, np.frexp(amax)[1] - 1 + 127, 0) - down, 1)
    scale = np.exp2(byte - 127.0)
    codes = (blocks / scale).astype(np.float32).astype(dtype).astype(np.float64)
    return np.moveaxis((codes * scale).reshape(v.shape), -1, axis)


WIDE = False


def mx_kscale(k):
    if not WIDE:
        return np.ones(k)
    levels = np.array([20, -20, 10, -10, 0])
    a = np.random.permutation(np.resize(levels, k // 512 * 4)).reshape(k // 512, 4)
    idx = np.arange(k)
    return np.exp2(a[idx // 512, idx % 128 // 32])


BF16 = ml_dtypes.bfloat16


def bf(x):
    return np.asarray(x, np.float32).astype(BF16)


def f64(x):
    return np.asarray(x).astype(np.float64)


B, C, H, W, K, R = 4, 512, 64, 64, 512, 8
N = B * H * W
EPS = 1e-8


def setup_inputs():
    s = mx_kscale(N).reshape(B, 1, H, W)
    core = np.random.standard_normal((R, C)) / np.sqrt(R)
    fa = np.random.standard_normal((B, R, H, W))
    pa = np.random.standard_normal((K, R))
    features = 0.5 * np.random.standard_normal((B, C, H, W))
    prototypes = 0.5 * np.random.standard_normal((K, C))
    for r in range(R):
        features += core[r][None, :, None, None] * fa[:, r][:, None]
        prototypes += pa[:, r][:, None] * core[r][None, :]
    g = np.random.standard_normal((B, K, H, W)) * np.exp2(np.random.randint(-12, 1, (B, 1, H, W)))
    return {"features": bf(features * s), "prototypes": bf(prototypes * 0.5 / np.sqrt(C)), "grad_out": bf(g)}


def reference(features, prototypes, grad_out):
    f = f64(features).reshape(B, C, H * W).transpose(0, 2, 1).reshape(N, C)
    g = f64(grad_out).reshape(B, K, H * W).transpose(0, 2, 1).reshape(N, K)
    p = f64(prototypes)
    f_norm = np.sqrt(np.sum(f * f, axis=1))
    p_norm = np.sqrt(np.sum(p * p, axis=1))
    gs = g / f_norm[:, None]
    m = mxq(gs, 0, "e5m2").T @ mxq(f, 0, "e4m3")
    proj = np.sum(m * p, axis=1)
    return m / p_norm[:, None] - p * (proj / p_norm ** 3)[:, None]

@@ -1,0 +1,214 @@
+from contextlib import ExitStack
+
+import concourse.mybir as mybir
+from concourse.masks import make_identity
+
+F32 = mybir.dt.float32
+BF16 = mybir.dt.bfloat16
+U32 = mybir.dt.uint32
+U8 = mybir.dt.uint8
+E4M3_X4 = mybir.dt.float8_e4m3fn_x4
+E5M2_X4 = mybir.dt.float8_e5m2_x4
+ACT = mybir.ActivationFunctionType
+ALU = mybir.AluOpType
+
+P = 128
+PACK = 4
+IMAGES, C, K, IMAGE_PIX = 4, 512, 512, 64 * 64
+ROW_TILES = 4
+PASS_PIX = P * PACK
+PASS_WORDS = PASS_PIX // 2
+N_PASS = IMAGES * IMAGE_PIX // PASS_PIX
+CHUNK_PASSES = 2
+CHUNK_PIX = CHUNK_PASSES * PASS_PIX
+N_CHUNK = N_PASS // CHUNK_PASSES
+ROW_BUFS = 4
+BANK_ROWS = 2 * P
+
+FLOPS = 2 * K * C * IMAGES * IMAGE_PIX
+
+
+def tile_globalprototype_kernel(tc, features, prototypes, grad_out, out):
+    nc = tc.nc
+    f_rows = features.rearrange("b (r p) h w -> b r p (h w)", p=P)
+    g_rows = grad_out.rearrange("b (r p) h w -> b r p (h w)", p=P)
+    out_rows = out.rearrange("(r p) c -> r p c", p=P)
+
+    with ExitStack() as ctx:
+        const = ctx.enter_context(tc.tile_pool(name="const", bufs=1))
+        rows = ctx.enter_context(tc.tile_pool(name="rows", bufs=ROW_BUFS))
+        groups = ctx.enter_context(tc.tile_pool(name="groups", bufs=3))
+        packed = ctx.enter_context(tc.tile_pool(name="packed", bufs=4))
+        small = ctx.enter_context(tc.tile_pool(name="small", bufs=4))
+        scratch = ctx.enter_context(tc.tile_pool(name="scratch", bufs=2))
+        turned = ctx.enter_context(tc.psum_pool(name="turned", bufs=1))
+        sums = ctx.enter_context(tc.psum_pool(name="sums", bufs=1))
+        ctx.enter_context(tc.manual_schedule())
+
+        identity = const.tile([P, P], F32, name="identity")
+        make_identity(nc, identity[:])
+        warm = const.tile([P, 1], F32, name="warm")
+        nc.vector.memset(warm[:], 1.0)
+        nc.scalar.activation(out=warm[:], in_=warm[:], func=ACT.Sqrt)
+
+        m_sums = [sums.tile([P, C], F32, name="m_sum%d" % r) for r in range(ROW_TILES)]
+
+        def load_chunk(dram_rows, name, chunk):
+            image, first = divmod(chunk * CHUNK_PIX, IMAGE_PIX)
+            raw = rows.tile([P, ROW_TILES, CHUNK_PIX], BF16, name=name)
+            for r in range(ROW_TILES):
+                nc.sync.dma_start(out=raw[:, r, :], in_=dram_rows[image, r, :, first : first + CHUNK_PIX])
+            return raw
+
+        def turn(raw_chunks, dram_rows, name, i):
+            chunk, part = divmod(i, CHUNK_PASSES)
+            words = raw_chunks[chunk][:].bitcast(F32)
+            banks = []
+            for h in range(ROW_TILES * P // BANK_ROWS):
+                bank = turned.tile([P, 2, BANK_ROWS], F32, name="%s_bank%d" % (name, h))
+                for u in range(2):
+                    first = part * PASS_WORDS + u * P
+                    for j in range(BANK_ROWS // P):
+                        nc.tensor.transpose(
+                            bank[:, u, j * P : (j + 1) * P],
+                            words[:, h * (BANK_ROWS // P) + j, first : first + P],
+                            identity[:],
+                        )
+                banks.append(bank)
+            if part == CHUNK_PASSES - 1 and chunk + ROW_BUFS < N_CHUNK:
+                raw_chunks[chunk + ROW_BUFS] = load_chunk(dram_rows, name, chunk + ROW_BUFS)
+            return banks
+
+        def regroup_features(banks):
+            grouped = groups.tile([P, C, PACK], BF16, name="f_grouped", align_bytes=64)
+            grouped_words = grouped[:].bitcast(F32)
+            for h, bank in enumerate(banks):
+                nc.scalar.copy(
+                    out=grouped_words[:, h * BANK_ROWS : (h + 1) * BANK_ROWS, :],
+                    in_=bank[:].rearrange("p u c -> p c u"),
+                )
+            return grouped
+
+        def sum_squares(grouped):
+            sumsq = small.tile([P, PACK], F32, name="sumsq")
+            squares = scratch.tile([P, PACK, C], BF16, name="squares")
+            for t in range(PACK):
+                nc.scalar.activation(
+                    out=squares[:, t, :], in_=grouped[:, :, t], func=ACT.Square, accum_out=sumsq[:, t : t + 1]
+                )
+            return sumsq
+
+        def inverse_norms(sumsq):
+            norm = small.tile([P, PACK], F32, name="norm")
+            nc.scalar.activation(out=norm[:], in_=sumsq[:], func=ACT.Sqrt)
+            inv_norm = small.tile([P, PACK], F32, name="inv_norm")
+            nc.vector.reciprocal(inv_norm[:], norm[:])
+            return inv_norm
+
+        def scale_gradients(banks, inv_norm):
+            gs = groups.tile([P, K, PACK], BF16, name="gs", align_bytes=64)
+            per_pixel = inv_norm[:].rearrange("p (u e) -> p u e", u=2).unsqueeze(1)
+            for h, bank in enumerate(banks):
+                nc.vector.tensor_tensor(
+                    out=gs[:, h * BANK_ROWS : (h + 1) * BANK_ROWS, :].rearrange("p k (u e) -> p k u e", u=2),
+                    in0=bank[:].bitcast(BF16).rearrange("p u (k e) -> p k u e", e=2),
+                    in1=per_pixel.to_broadcast([P, BANK_ROWS, 2, 2]),
+                    op=ALU.mult,
+                )
+            return gs
+
+        def quantise(grouped, width, fmt, name):
+            codes = packed.tile([P, width], U32, name=name + "_codes", align_bytes=64)
+            scales = packed.tile([P, width], U8, name=name + "_scales", align_bytes=64)
+            nc.vector.quantize_mx(
+                out=codes[:].bitcast(fmt), scales=scales[:], in_=grouped[:].rearrange("p w t -> p (w t)")
+            )
+            return codes, scales
+
+        def multiply(i, g_mx, f_mx, row_tiles):
+            g_codes, g_scales = g_mx
+            f_codes, f_scales = f_mx
+            for r in row_tiles:
+                k_cols = slice(r * P, (r + 1) * P)
+                nc.tensor.matmul_mx(
+                    out=m_sums[r][:],
+                    lhsT=g_codes[:, k_cols].bitcast(E5M2_X4),
+                    lhsT_scale=g_scales[:, k_cols],
+                    rhs=f_codes[:].bitcast(E4M3_X4),
+                    rhs_scale=f_scales[:],
+                    start=(i == 0),
+                    stop=(i == N_PASS - 1),
+                )
+
+        f_raw, g_raw = {}, {}
+        for chunk in range(ROW_BUFS):
+            f_raw[chunk] = load_chunk(f_rows, "f", chunk)
+            g_raw[chunk] = load_chunk(g_rows, "g", chunk)
+        protos = const.tile([P, ROW_TILES, C], BF16, name="protos")
+        nc.sync.dma_start(out=protos[:], in_=prototypes.rearrange("(r p) c -> p r c", p=P))
+
+        f_banks, g_banks, f_grouped, sumsq, gs, f_mx, g_mx = {}, {}, {}, {}, {}, {}, {}
+        f_banks[0] = turn(f_raw, f_rows, "f", 0)
+        for i in range(N_PASS + 2):
+            if i < N_PASS:
+                f_grouped[i] = regroup_features(f_banks[i])
+            if i + 1 < N_PASS:
+                f_banks[i + 1] = turn(f_raw, f_rows, "f", i + 1)
+            if i >= 2:
+                multiply(i - 2, g_mx[i - 2], f_mx[i - 2], (0, 1))
+            if 1 <= i <= N_PASS:
+                gs[i - 1] = scale_gradients(g_banks[i - 1], inverse_norms(sumsq[i - 1]))
+            if i < N_PASS:
+                g_banks[i] = turn(g_raw, g_rows, "g", i)
+            if i >= 2:
+                multiply(i - 2, g_mx[i - 2], f_mx[i - 2], (2, 3))
+            if i < N_PASS:
+                sumsq[i] = sum_squares(f_grouped[i])
+                f_mx[i] = quantise(f_grouped[i], C, E4M3_X4, "f")
+            if 1 <= i <= N_PASS:
+                g_mx[i - 1] = quantise(gs[i - 1], K, E5M2_X4, "g")
+
+        p_sumsq = const.tile([P, ROW_TILES], F32, name="p_sumsq")
+        p_squares = const.tile([P, ROW_TILES, C], BF16, name="p_squares")
+        for r in range(ROW_TILES):
+            nc.scalar.activation(
+                out=p_squares[:, r, :], in_=protos[:, r, :], func=ACT.Square, accum_out=p_sumsq[:, r : r + 1]
+            )
+        p_norm = const.tile([P, ROW_TILES], F32, name="p_norm")
+        nc.scalar.activation(out=p_norm[:], in_=p_sumsq[:], func=ACT.Sqrt)
+        inv_p = const.tile([P, ROW_TILES], F32, name="inv_p")
+        nc.vector.reciprocal(inv_p[:], p_norm[:])
+        inv_p2 = const.tile([P, ROW_TILES], F32, name="inv_p2")
+        nc.vector.tensor_mul(inv_p2[:], inv_p[:], inv_p[:])
+        neg_inv_p3 = const.tile([P, ROW_TILES], F32, name="neg_inv_p3")
+        nc.vector.scalar_tensor_tensor(
+            out=neg_inv_p3[:], in0=inv_p2[:], scalar=-1.0, in1=inv_p[:], op0=ALU.mult, op1=ALU.mult
+        )
+
+        proj = const.tile([P, ROW_TILES], F32, name="proj")
+        products = const.tile([P, ROW_TILES, C], F32, name="products")
+        m_scaled = const.tile([P, ROW_TILES, C], F32, name="m_scaled")
+        result = const.tile([P, ROW_TILES, C], F32, name="result")
+        for r in range(ROW_TILES):
+            nc.vector.scalar_tensor_tensor(
+                out=products[:, r, :],
+                in0=m_sums[r][:],
+                scalar=1.0,
+                in1=protos[:, r, :],
+                op0=ALU.mult,
+                op1=ALU.mult,
+                accum_out=proj[:, r : r + 1],
+            )
+            nc.scalar.activation(out=m_scaled[:, r, :], in_=m_sums[r][:], func=ACT.Copy, scale=inv_p[:, r : r + 1])
+        pull = const.tile([P, ROW_TILES], F32, name="pull")
+        nc.vector.tensor_mul(pull[:], proj[:], neg_inv_p3[:])
+        for r in range(ROW_TILES):
+            nc.vector.scalar_tensor_tensor(
+                out=result[:, r, :],
+                in0=protos[:, r, :],
+                scalar=pull[:, r : r + 1],
+                in1=m_scaled[:, r, :],
+                op0=ALU.mult,
+                op1=ALU.add,
+            )
+            nc.sync.dma_start(out=out_rows[r], in_=result[:, r, :])

@@ -47,9 +47,10 @@ def tile_globalprototype_kernel(tc, features, prototypes, grad_out, out):
 
         identity = const.tile([P, P], F32, name="identity")
         make_identity(nc, identity[:])
-        warm = const.tile([P, 1], F32, name="warm")
-        nc.vector.memset(warm[:], 1.0)
-        nc.scalar.activation(out=warm[:], in_=warm[:], func=ACT.Sqrt)
+        minus_half = const.tile([P, PACK], F32, name="minus_half")
+        nc.gpsimd.memset(minus_half[:], -0.5)
+        minus_three_halves = const.tile([P, ROW_TILES], F32, name="minus_three_halves")
+        nc.gpsimd.memset(minus_three_halves[:], -1.5)
 
         m_sums = [sums.tile([P, C], F32, name="m_sum%d" % r) for r in range(ROW_TILES)]
 
@@ -89,20 +90,15 @@ def tile_globalprototype_kernel(tc, features, prototypes, grad_out, out):
                 )
             return grouped
 
-        def sum_squares(grouped):
+        def inverse_norms(grouped):
             sumsq = small.tile([P, PACK], F32, name="sumsq")
             squares = scratch.tile([P, PACK, C], BF16, name="squares")
             for t in range(PACK):
                 nc.scalar.activation(
                     out=squares[:, t, :], in_=grouped[:, :, t], func=ACT.Square, accum_out=sumsq[:, t : t + 1]
                 )
-            return sumsq
-
-        def inverse_norms(sumsq):
-            norm = small.tile([P, PACK], F32, name="norm")
-            nc.scalar.activation(out=norm[:], in_=sumsq[:], func=ACT.Sqrt)
             inv_norm = small.tile([P, PACK], F32, name="inv_norm")
-            nc.vector.reciprocal(inv_norm[:], norm[:])
+            nc.gpsimd.tensor_tensor(out=inv_norm[:], in0=sumsq[:], in1=minus_half[:], op=ALU.pow)
             return inv_norm
 
         def scale_gradients(banks, inv_norm):
@@ -147,26 +143,30 @@ def tile_globalprototype_kernel(tc, features, prototypes, grad_out, out):
         protos = const.tile([P, ROW_TILES, C], BF16, name="protos")
         nc.sync.dma_start(out=protos[:], in_=prototypes.rearrange("(r p) c -> p r c", p=P))
 
-        f_banks, g_banks, f_grouped, sumsq, gs, f_mx, g_mx = {}, {}, {}, {}, {}, {}, {}
+        def is_pass(j):
+            return 0 <= j < N_PASS
+
+        f_banks, g_banks, f_grouped, inv_norm, gs, f_mx, g_mx = {}, {}, {}, {}, {}, {}, {}
         f_banks[0] = turn(f_raw, f_rows, "f", 0)
-        for i in range(N_PASS + 2):
-            if i < N_PASS:
+        for i in range(N_PASS + 3):
+            if is_pass(i):
                 f_grouped[i] = regroup_features(f_banks[i])
-            if i + 1 < N_PASS:
+            if is_pass(i + 1):
                 f_banks[i + 1] = turn(f_raw, f_rows, "f", i + 1)
-            if i >= 2:
-                multiply(i - 2, g_mx[i - 2], f_mx[i - 2], (0, 1))
-            if 1 <= i <= N_PASS:
-                gs[i - 1] = scale_gradients(g_banks[i - 1], inverse_norms(sumsq[i - 1]))
-            if i < N_PASS:
-                g_banks[i] = turn(g_raw, g_rows, "g", i)
-            if i >= 2:
-                multiply(i - 2, g_mx[i - 2], f_mx[i - 2], (2, 3))
-            if i < N_PASS:
-                sumsq[i] = sum_squares(f_grouped[i])
-                f_mx[i] = quantise(f_grouped[i], C, E4M3_X4, "f")
-            if 1 <= i <= N_PASS:
-                g_mx[i - 1] = quantise(gs[i - 1], K, E5M2_X4, "g")
+            if is_pass(i - 3):
+                multiply(i - 3, g_mx[i - 3], f_mx[i - 3], (0, 1))
+            if is_pass(i - 1):
+                inv_norm[i - 1] = inverse_norms(f_grouped[i - 1])
+            if is_pass(i - 2):
+                gs[i - 2] = scale_gradients(g_banks[i - 2], inv_norm[i - 2])
+            if is_pass(i - 1):
+                g_banks[i - 1] = turn(g_raw, g_rows, "g", i - 1)
+            if is_pass(i - 3):
+                multiply(i - 3, g_mx[i - 3], f_mx[i - 3], (2, 3))
+            if is_pass(i - 1):
+                f_mx[i - 1] = quantise(f_grouped[i - 1], C, E4M3_X4, "f")
+            if is_pass(i - 2):
+                g_mx[i - 2] = quantise(gs[i - 2], K, E5M2_X4, "g")
 
         p_sumsq = const.tile([P, ROW_TILES], F32, name="p_sumsq")
         p_squares = const.tile([P, ROW_TILES, C], BF16, name="p_squares")
@@ -174,16 +174,10 @@ def tile_globalprototype_kernel(tc, features, prototypes, grad_out, out):
             nc.scalar.activation(
                 out=p_squares[:, r, :], in_=protos[:, r, :], func=ACT.Square, accum_out=p_sumsq[:, r : r + 1]
             )
-        p_norm = const.tile([P, ROW_TILES], F32, name="p_norm")
-        nc.scalar.activation(out=p_norm[:], in_=p_sumsq[:], func=ACT.Sqrt)
         inv_p = const.tile([P, ROW_TILES], F32, name="inv_p")
-        nc.vector.reciprocal(inv_p[:], p_norm[:])
-        inv_p2 = const.tile([P, ROW_TILES], F32, name="inv_p2")
-        nc.vector.tensor_mul(inv_p2[:], inv_p[:], inv_p[:])
-        neg_inv_p3 = const.tile([P, ROW_TILES], F32, name="neg_inv_p3")
-        nc.vector.scalar_tensor_tensor(
-            out=neg_inv_p3[:], in0=inv_p2[:], scalar=-1.0, in1=inv_p[:], op0=ALU.mult, op1=ALU.mult
-        )
+        nc.gpsimd.tensor_tensor(out=inv_p[:], in0=p_sumsq[:], in1=minus_half[:], op=ALU.pow)
+        inv_p3 = const.tile([P, ROW_TILES], F32, name="inv_p3")
+        nc.gpsimd.tensor_tensor(out=inv_p3[:], in0=p_sumsq[:], in1=minus_three_halves[:], op=ALU.pow)
 
         proj = const.tile([P, ROW_TILES], F32, name="proj")
         products = const.tile([P, ROW_TILES, C], F32, name="products")
@@ -201,7 +195,9 @@ def tile_globalprototype_kernel(tc, features, prototypes, grad_out, out):
             )
             nc.scalar.activation(out=m_scaled[:, r, :], in_=m_sums[r][:], func=ACT.Copy, scale=inv_p[:, r : r + 1])
         pull = const.tile([P, ROW_TILES], F32, name="pull")
-        nc.vector.tensor_mul(pull[:], proj[:], neg_inv_p3[:])
+        nc.vector.scalar_tensor_tensor(
+            out=pull[:], in0=proj[:], scalar=-1.0, in1=inv_p3[:], op0=ALU.mult, op1=ALU.mult
+        )
         for r in range(ROW_TILES):
             nc.vector.scalar_tensor_tensor(
                 out=result[:, r, :],

@@ -24,6 +24,7 @@ CHUNK_PIX = CHUNK_PASSES * PASS_PIX
 N_CHUNK = N_PASS // CHUNK_PASSES
 ROW_BUFS = 4
 BANK_ROWS = 2 * P
+VECTOR_CHANNELS = 96
 
 FLOPS = 2 * K * C * IMAGES * IMAGE_PIX
 
@@ -84,10 +85,17 @@ def tile_globalprototype_kernel(tc, features, prototypes, grad_out, out):
             grouped = groups.tile([P, C, PACK], BF16, name="f_grouped", align_bytes=64)
             grouped_words = grouped[:].bitcast(F32)
             for h, bank in enumerate(banks):
+                first = h * BANK_ROWS
+                split = min((h + 1) * BANK_ROWS, C - VECTOR_CHANNELS)
                 nc.scalar.copy(
-                    out=grouped_words[:, h * BANK_ROWS : (h + 1) * BANK_ROWS, :],
-                    in_=bank[:].rearrange("p u c -> p c u"),
+                    out=grouped_words[:, first:split, :],
+                    in_=bank[:, :, : split - first].rearrange("p u c -> p c u"),
                 )
+                if split < (h + 1) * BANK_ROWS:
+                    nc.vector.tensor_copy(
+                        out=grouped_words[:, split : (h + 1) * BANK_ROWS, :],
+                        in_=bank[:, :, split - first :].rearrange("p u c -> p c u"),
+                    )
             return grouped
 
         def inverse_norms(grouped):

@@ -24,7 +24,7 @@ CHUNK_PIX = CHUNK_PASSES * PASS_PIX
 N_CHUNK = N_PASS // CHUNK_PASSES
 ROW_BUFS = 4
 BANK_ROWS = 2 * P
-VECTOR_CHANNELS = 96
+GPSIMD_ROWS = 192
 
 FLOPS = 2 * K * C * IMAGES * IMAGE_PIX
 
@@ -38,10 +38,10 @@ def tile_globalprototype_kernel(tc, features, prototypes, grad_out, out):
     with ExitStack() as ctx:
         const = ctx.enter_context(tc.tile_pool(name="const", bufs=1))
         rows = ctx.enter_context(tc.tile_pool(name="rows", bufs=ROW_BUFS))
-        groups = ctx.enter_context(tc.tile_pool(name="groups", bufs=3))
+        groups = ctx.enter_context(tc.tile_pool(name="groups", bufs=5))
         packed = ctx.enter_context(tc.tile_pool(name="packed", bufs=4))
         small = ctx.enter_context(tc.tile_pool(name="small", bufs=4))
-        scratch = ctx.enter_context(tc.tile_pool(name="scratch", bufs=2))
+        scratch = ctx.enter_context(tc.tile_pool(name="scratch", bufs=4))
         turned = ctx.enter_context(tc.psum_pool(name="turned", bufs=1))
         sums = ctx.enter_context(tc.psum_pool(name="sums", bufs=1))
         ctx.enter_context(tc.manual_schedule())
@@ -85,38 +85,48 @@ def tile_globalprototype_kernel(tc, features, prototypes, grad_out, out):
             grouped = groups.tile([P, C, PACK], BF16, name="f_grouped", align_bytes=64)
             grouped_words = grouped[:].bitcast(F32)
             for h, bank in enumerate(banks):
-                first = h * BANK_ROWS
-                split = min((h + 1) * BANK_ROWS, C - VECTOR_CHANNELS)
-                nc.scalar.copy(
-                    out=grouped_words[:, first:split, :],
-                    in_=bank[:, :, : split - first].rearrange("p u c -> p c u"),
+                copy = (nc.scalar.copy, nc.vector.tensor_copy)[h]
+                copy(
+                    out=grouped_words[:, h * BANK_ROWS : (h + 1) * BANK_ROWS, :],
+                    in_=bank[:].rearrange("p u c -> p c u"),
                 )
-                if split < (h + 1) * BANK_ROWS:
-                    nc.vector.tensor_copy(
-                        out=grouped_words[:, split : (h + 1) * BANK_ROWS, :],
-                        in_=bank[:, :, split - first :].rearrange("p u c -> p c u"),
-                    )
             return grouped
 
-        def inverse_norms(grouped):
-            sumsq = small.tile([P, PACK], F32, name="sumsq")
-            squares = scratch.tile([P, PACK, C], BF16, name="squares")
-            for t in range(PACK):
+        def sum_squares(grouped, sumsq, slots):
+            for t in slots:
+                squares = scratch.tile([P, C], BF16, name="squares")
                 nc.scalar.activation(
-                    out=squares[:, t, :], in_=grouped[:, :, t], func=ACT.Square, accum_out=sumsq[:, t : t + 1]
+                    out=squares[:], in_=grouped[:, :, t], func=ACT.Square, accum_out=sumsq[:, t : t + 1]
                 )
+
+        def inverse_norms(sumsq):
             inv_norm = small.tile([P, PACK], F32, name="inv_norm")
             nc.gpsimd.tensor_tensor(out=inv_norm[:], in0=sumsq[:], in1=minus_half[:], op=ALU.pow)
             return inv_norm
 
-        def scale_gradients(banks, inv_norm):
+        def regroup_share(banks):
+            raw = groups.tile([P, GPSIMD_ROWS, PACK], BF16, name="g_share", align_bytes=64)
+            nc.scalar.copy(
+                out=raw[:].bitcast(F32), in_=banks[-1][:, :, BANK_ROWS - GPSIMD_ROWS :].rearrange("p u k -> p k u")
+            )
+            return raw
+
+        def scale_gradients(banks, share, inv_norm):
             gs = groups.tile([P, K, PACK], BF16, name="gs", align_bytes=64)
             per_pixel = inv_norm[:].rearrange("p (u e) -> p u e", u=2).unsqueeze(1)
+            nc.gpsimd.tensor_tensor(
+                out=gs[:, K - GPSIMD_ROWS :, :],
+                in0=share[:],
+                in1=inv_norm[:].unsqueeze(1).to_broadcast([P, GPSIMD_ROWS, PACK]),
+                op=ALU.mult,
+            )
             for h, bank in enumerate(banks):
+                first = h * BANK_ROWS
+                count = min(BANK_ROWS, K - GPSIMD_ROWS - first)
                 nc.vector.tensor_tensor(
-                    out=gs[:, h * BANK_ROWS : (h + 1) * BANK_ROWS, :].rearrange("p k (u e) -> p k u e", u=2),
-                    in0=bank[:].bitcast(BF16).rearrange("p u (k e) -> p k u e", e=2),
-                    in1=per_pixel.to_broadcast([P, BANK_ROWS, 2, 2]),
+                    out=gs[:, first : first + count, :].rearrange("p k (u e) -> p k u e", u=2),
+                    in0=bank[:].bitcast(BF16).rearrange("p u (k e) -> p k u e", e=2)[:, :count],
+                    in1=per_pixel.to_broadcast([P, count, 2, 2]),
                     op=ALU.mult,
                 )
             return gs
@@ -154,27 +164,30 @@ def tile_globalprototype_kernel(tc, features, prototypes, grad_out, out):
         def is_pass(j):
             return 0 <= j < N_PASS
 
-        f_banks, g_banks, f_grouped, inv_norm, gs, f_mx, g_mx = {}, {}, {}, {}, {}, {}, {}
-        f_banks[0] = turn(f_raw, f_rows, "f", 0)
-        for i in range(N_PASS + 3):
+        f_banks, g_banks, f_grouped, sumsq, g_share, inv_norm, gs, f_mx, g_mx = {}, {}, {}, {}, {}, {}, {}, {}, {}
+        for i in range(-4, N_PASS + 1):
             if is_pass(i):
-                f_grouped[i] = regroup_features(f_banks[i])
+                gs[i] = scale_gradients(g_banks[i], g_share[i], inv_norm[i])
             if is_pass(i + 1):
-                f_banks[i + 1] = turn(f_raw, f_rows, "f", i + 1)
-            if is_pass(i - 3):
-                multiply(i - 3, g_mx[i - 3], f_mx[i - 3], (0, 1))
+                inv_norm[i + 1] = inverse_norms(sumsq[i + 1])
+            if is_pass(i + 3):
+                f_grouped[i + 3] = regroup_features(f_banks[i + 3])
+            if is_pass(i + 2):
+                sumsq[i + 2] = small.tile([P, PACK], F32, name="sumsq")
+                sum_squares(f_grouped[i + 2], sumsq[i + 2], (0, 1))
+            if is_pass(i + 1):
+                g_banks[i + 1] = turn(g_raw, g_rows, "g", i + 1)
+                g_share[i + 1] = regroup_share(g_banks[i + 1])
+            if is_pass(i + 2):
+                sum_squares(f_grouped[i + 2], sumsq[i + 2], (2, 3))
+            if is_pass(i + 1):
+                f_mx[i + 1] = quantise(f_grouped[i + 1], C, E4M3_X4, "f")
+            if is_pass(i):
+                g_mx[i] = quantise(gs[i], K, E5M2_X4, "g")
             if is_pass(i - 1):
-                inv_norm[i - 1] = inverse_norms(f_grouped[i - 1])
-            if is_pass(i - 2):
-                gs[i - 2] = scale_gradients(g_banks[i - 2], inv_norm[i - 2])
-            if is_pass(i - 1):
-                g_banks[i - 1] = turn(g_raw, g_rows, "g", i - 1)
-            if is_pass(i - 3):
-                multiply(i - 3, g_mx[i - 3], f_mx[i - 3], (2, 3))
-            if is_pass(i - 1):
-                f_mx[i - 1] = quantise(f_grouped[i - 1], C, E4M3_X4, "f")
-            if is_pass(i - 2):
-                g_mx[i - 2] = quantise(gs[i - 2], K, E5M2_X4, "g")
+                multiply(i - 1, g_mx[i - 1], f_mx[i - 1], range(ROW_TILES))
+            if is_pass(i + 4):
+                f_banks[i + 4] = turn(f_raw, f_rows, "f", i + 4)
 
         p_sumsq = const.tile([P, ROW_TILES], F32, name="p_sumsq")
         p_squares = const.tile([P, ROW_TILES, C], BF16, name="p_squares")

@@ -24,7 +24,8 @@ CHUNK_PIX = CHUNK_PASSES * PASS_PIX
 N_CHUNK = N_PASS // CHUNK_PASSES
 ROW_BUFS = 4
 BANK_ROWS = 2 * P
-GPSIMD_ROWS = 192
+
+VECTOR_COPIES = 3
 
 FLOPS = 2 * K * C * IMAGES * IMAGE_PIX
 
@@ -46,6 +47,9 @@ def tile_globalprototype_kernel(tc, features, prototypes, grad_out, out):
         sums = ctx.enter_context(tc.psum_pool(name="sums", bufs=1))
         ctx.enter_context(tc.manual_schedule())
 
+        warm = const.tile([P, 1], F32, name="warm")
+        nc.vector.memset(warm[:], 1.0)
+        nc.scalar.activation(out=warm[:], in_=warm[:], func=ACT.Sqrt)
         identity = const.tile([P, P], F32, name="identity")
         make_identity(nc, identity[:])
         minus_half = const.tile([P, PACK], F32, name="minus_half")
@@ -81,15 +85,16 @@ def tile_globalprototype_kernel(tc, features, prototypes, grad_out, out):
                 raw_chunks[chunk + ROW_BUFS] = load_chunk(dram_rows, name, chunk + ROW_BUFS)
             return banks
 
-        def regroup_features(banks):
+        def regroup_features(banks, copy, between):
             grouped = groups.tile([P, C, PACK], BF16, name="f_grouped", align_bytes=64)
             grouped_words = grouped[:].bitcast(F32)
             for h, bank in enumerate(banks):
-                copy = (nc.scalar.copy, nc.vector.tensor_copy)[h]
                 copy(
                     out=grouped_words[:, h * BANK_ROWS : (h + 1) * BANK_ROWS, :],
                     in_=bank[:].rearrange("p u c -> p c u"),
                 )
+                if h == 0:
+                    between()
             return grouped
 
         def sum_squares(grouped, sumsq, slots):
@@ -99,34 +104,24 @@ def tile_globalprototype_kernel(tc, features, prototypes, grad_out, out):
                     out=squares[:], in_=grouped[:, :, t], func=ACT.Square, accum_out=sumsq[:, t : t + 1]
                 )
 
-        def inverse_norms(sumsq):
+        def roots(sumsq):
+            norm = small.tile([P, PACK], F32, name="norm")
+            nc.scalar.activation(out=norm[:], in_=sumsq[:], func=ACT.Sqrt)
+            return norm
+
+        def inverse_norms(norm):
             inv_norm = small.tile([P, PACK], F32, name="inv_norm")
-            nc.gpsimd.tensor_tensor(out=inv_norm[:], in0=sumsq[:], in1=minus_half[:], op=ALU.pow)
+            nc.vector.reciprocal(out=inv_norm[:], in_=norm[:])
             return inv_norm
 
-        def regroup_share(banks):
-            raw = groups.tile([P, GPSIMD_ROWS, PACK], BF16, name="g_share", align_bytes=64)
-            nc.scalar.copy(
-                out=raw[:].bitcast(F32), in_=banks[-1][:, :, BANK_ROWS - GPSIMD_ROWS :].rearrange("p u k -> p k u")
-            )
-            return raw
-
-        def scale_gradients(banks, share, inv_norm):
+        def scale_gradients(banks, inv_norm):
             gs = groups.tile([P, K, PACK], BF16, name="gs", align_bytes=64)
             per_pixel = inv_norm[:].rearrange("p (u e) -> p u e", u=2).unsqueeze(1)
-            nc.gpsimd.tensor_tensor(
-                out=gs[:, K - GPSIMD_ROWS :, :],
-                in0=share[:],
-                in1=inv_norm[:].unsqueeze(1).to_broadcast([P, GPSIMD_ROWS, PACK]),
-                op=ALU.mult,
-            )
             for h, bank in enumerate(banks):
-                first = h * BANK_ROWS
-                count = min(BANK_ROWS, K - GPSIMD_ROWS - first)
                 nc.vector.tensor_tensor(
-                    out=gs[:, first : first + count, :].rearrange("p k (u e) -> p k u e", u=2),
-                    in0=bank[:].bitcast(BF16).rearrange("p u (k e) -> p k u e", e=2)[:, :count],
-                    in1=per_pixel.to_broadcast([P, count, 2, 2]),
+                    out=gs[:, h * BANK_ROWS : (h + 1) * BANK_ROWS, :].rearrange("p k (u e) -> p k u e", u=2),
+                    in0=bank[:].bitcast(BF16).rearrange("p u (k e) -> p k u e", e=2),
+                    in1=per_pixel.to_broadcast([P, BANK_ROWS, 2, 2]),
                     op=ALU.mult,
                 )
             return gs
@@ -164,23 +159,30 @@ def tile_globalprototype_kernel(tc, features, prototypes, grad_out, out):
         def is_pass(j):
             return 0 <= j < N_PASS
 
-        f_banks, g_banks, f_grouped, sumsq, g_share, inv_norm, gs, f_mx, g_mx = {}, {}, {}, {}, {}, {}, {}, {}, {}
+        f_banks, g_banks, f_grouped, sumsq, norm, inv_norm, gs, f_mx, g_mx = {}, {}, {}, {}, {}, {}, {}, {}, {}
+
+        def take_roots(j):
+            if is_pass(j):
+                norm[j] = roots(sumsq[j])
+
         for i in range(-4, N_PASS + 1):
             if is_pass(i):
-                gs[i] = scale_gradients(g_banks[i], g_share[i], inv_norm[i])
-            if is_pass(i + 1):
-                inv_norm[i + 1] = inverse_norms(sumsq[i + 1])
+                gs[i] = scale_gradients(g_banks[i], inv_norm[i])
             if is_pass(i + 3):
-                f_grouped[i + 3] = regroup_features(f_banks[i + 3])
+                f_grouped[i + 3] = regroup_features(
+                    f_banks[i + 3],
+                    nc.vector.tensor_copy if i + 3 < VECTOR_COPIES else nc.scalar.copy,
+                    lambda: take_roots(i + 1),
+                )
+            else:
+                take_roots(i + 1)
+            if is_pass(i + 1):
+                inv_norm[i + 1] = inverse_norms(norm[i + 1])
             if is_pass(i + 2):
                 sumsq[i + 2] = small.tile([P, PACK], F32, name="sumsq")
-                sum_squares(f_grouped[i + 2], sumsq[i + 2], (0, 1))
+                sum_squares(f_grouped[i + 2], sumsq[i + 2], range(PACK))
             if is_pass(i + 1):
                 g_banks[i + 1] = turn(g_raw, g_rows, "g", i + 1)
-                g_share[i + 1] = regroup_share(g_banks[i + 1])
-            if is_pass(i + 2):
-                sum_squares(f_grouped[i + 2], sumsq[i + 2], (2, 3))
-            if is_pass(i + 1):
                 f_mx[i + 1] = quantise(f_grouped[i + 1], C, E4M3_X4, "f")
             if is_pass(i):
                 g_mx[i] = quantise(gs[i], K, E5M2_X4, "g")
@@ -201,31 +203,43 @@ def tile_globalprototype_kernel(tc, features, prototypes, grad_out, out):
         nc.gpsimd.tensor_tensor(out=inv_p3[:], in0=p_sumsq[:], in1=minus_three_halves[:], op=ALU.pow)
 
         proj = const.tile([P, ROW_TILES], F32, name="proj")
+        pull = const.tile([P, ROW_TILES], F32, name="pull")
         products = const.tile([P, ROW_TILES, C], F32, name="products")
         m_scaled = const.tile([P, ROW_TILES, C], F32, name="m_scaled")
         result = const.tile([P, ROW_TILES, C], F32, name="result")
-        for r in range(ROW_TILES):
-            nc.vector.scalar_tensor_tensor(
-                out=products[:, r, :],
-                in0=m_sums[r][:],
-                scalar=1.0,
-                in1=protos[:, r, :],
-                op0=ALU.mult,
-                op1=ALU.mult,
-                accum_out=proj[:, r : r + 1],
-            )
-            nc.scalar.activation(out=m_scaled[:, r, :], in_=m_sums[r][:], func=ACT.Copy, scale=inv_p[:, r : r + 1])
-        pull = const.tile([P, ROW_TILES], F32, name="pull")
-        nc.vector.scalar_tensor_tensor(
-            out=pull[:], in0=proj[:], scalar=-1.0, in1=inv_p3[:], op0=ALU.mult, op1=ALU.mult
-        )
-        for r in range(ROW_TILES):
-            nc.vector.scalar_tensor_tensor(
-                out=result[:, r, :],
-                in0=protos[:, r, :],
-                scalar=pull[:, r : r + 1],
-                in1=m_scaled[:, r, :],
-                op0=ALU.mult,
-                op1=ALU.add,
-            )
-            nc.sync.dma_start(out=out_rows[r], in_=result[:, r, :])
+        for step in range(ROW_TILES + 2):
+            r = step
+            if r < ROW_TILES:
+                nc.vector.scalar_tensor_tensor(
+                    out=products[:, r, :],
+                    in0=m_sums[r][:],
+                    scalar=1.0,
+                    in1=protos[:, r, :],
+                    op0=ALU.mult,
+                    op1=ALU.mult,
+                    accum_out=proj[:, r : r + 1],
+                )
+                nc.scalar.activation(
+                    out=m_scaled[:, r, :], in_=m_sums[r][:], func=ACT.Copy, scale=inv_p[:, r : r + 1]
+                )
+            r = step - 1
+            if 0 <= r < ROW_TILES:
+                nc.vector.scalar_tensor_tensor(
+                    out=pull[:, r : r + 1],
+                    in0=proj[:, r : r + 1],
+                    scalar=-1.0,
+                    in1=inv_p3[:, r : r + 1],
+                    op0=ALU.mult,
+                    op1=ALU.mult,
+                )
+            r = step - 2
+            if r >= 0:
+                nc.vector.scalar_tensor_tensor(
+                    out=result[:, r, :],
+                    in0=protos[:, r, :],
+                    scalar=pull[:, r : r + 1],
+                    in1=m_scaled[:, r, :],
+                    op0=ALU.mult,
+                    op1=ALU.add,
+                )
+                nc.sync.dma_start(out=out_rows[r], in_=result[:, r, :])

@@ -181,13 +181,15 @@ def tile_globalprototype_kernel(tc, features, prototypes, grad_out, out):
             if is_pass(i + 2):
                 sumsq[i + 2] = small.tile([P, PACK], F32, name="sumsq")
                 sum_squares(f_grouped[i + 2], sumsq[i + 2], range(PACK))
+            if is_pass(i - 1):
+                multiply(i - 1, g_mx[i - 1], f_mx[i - 1], (0, 1))
             if is_pass(i + 1):
                 g_banks[i + 1] = turn(g_raw, g_rows, "g", i + 1)
                 f_mx[i + 1] = quantise(f_grouped[i + 1], C, E4M3_X4, "f")
             if is_pass(i):
                 g_mx[i] = quantise(gs[i], K, E5M2_X4, "g")
             if is_pass(i - 1):
-                multiply(i - 1, g_mx[i - 1], f_mx[i - 1], range(ROW_TILES))
+                multiply(i - 1, g_mx[i - 1], f_mx[i - 1], (2, 3))
             if is_pass(i + 4):
                 f_banks[i + 4] = turn(f_raw, f_rows, "f", i + 4)
 

@@ -22,10 +22,12 @@ N_PASS = IMAGES * IMAGE_PIX // PASS_PIX
 CHUNK_PASSES = 2
 CHUNK_PIX = CHUNK_PASSES * PASS_PIX
 N_CHUNK = N_PASS // CHUNK_PASSES
-ROW_BUFS = 4
+ROW_BUFS = 5
 BANK_ROWS = 2 * P
 
-VECTOR_COPIES = 3
+
+SHARE_ROWS = 64
+FAR_BELOW = -(2.0**126)
 
 FLOPS = 2 * K * C * IMAGES * IMAGE_PIX
 
@@ -40,7 +42,7 @@ def tile_globalprototype_kernel(tc, features, prototypes, grad_out, out):
         const = ctx.enter_context(tc.tile_pool(name="const", bufs=1))
         rows = ctx.enter_context(tc.tile_pool(name="rows", bufs=ROW_BUFS))
         groups = ctx.enter_context(tc.tile_pool(name="groups", bufs=5))
-        packed = ctx.enter_context(tc.tile_pool(name="packed", bufs=4))
+        packed = ctx.enter_context(tc.tile_pool(name="packed", bufs=6))
         small = ctx.enter_context(tc.tile_pool(name="small", bufs=4))
         scratch = ctx.enter_context(tc.tile_pool(name="scratch", bufs=4))
         turned = ctx.enter_context(tc.psum_pool(name="turned", bufs=1))
@@ -52,6 +54,12 @@ def tile_globalprototype_kernel(tc, features, prototypes, grad_out, out):
         nc.scalar.activation(out=warm[:], in_=warm[:], func=ACT.Sqrt)
         identity = const.tile([P, P], F32, name="identity")
         make_identity(nc, identity[:])
+        identity_bf16 = const.tile([P, P], BF16, name="identity_bf16")
+        nc.vector.tensor_copy(out=identity_bf16[:], in_=identity[:])
+        off_diagonal = const.tile([P, P], BF16, name="off_diagonal")
+        nc.vector.tensor_scalar(
+            out=off_diagonal[:], in0=identity[:], scalar1=-FAR_BELOW, scalar2=FAR_BELOW, op0=ALU.mult, op1=ALU.add
+        )
         minus_half = const.tile([P, PACK], F32, name="minus_half")
         nc.gpsimd.memset(minus_half[:], -0.5)
         minus_three_halves = const.tile([P, ROW_TILES], F32, name="minus_three_halves")
@@ -59,49 +67,75 @@ def tile_globalprototype_kernel(tc, features, prototypes, grad_out, out):
 
         m_sums = [sums.tile([P, C], F32, name="m_sum%d" % r) for r in range(ROW_TILES)]
 
-        def load_chunk(dram_rows, name, chunk):
+        def new_chunk(name):
+            return rows.tile([P, ROW_TILES, CHUNK_PIX], BF16, name=name)
+
+        def load(raw, dram_rows, chunk, pixels):
             image, first = divmod(chunk * CHUNK_PIX, IMAGE_PIX)
-            raw = rows.tile([P, ROW_TILES, CHUNK_PIX], BF16, name=name)
             for r in range(ROW_TILES):
-                nc.sync.dma_start(out=raw[:, r, :], in_=dram_rows[image, r, :, first : first + CHUNK_PIX])
+                nc.sync.dma_start(
+                    out=raw[:, r, pixels], in_=dram_rows[image, r, :, first + pixels.start : first + pixels.stop]
+                )
+
+        def load_chunk(dram_rows, name, chunk):
+            raw = new_chunk(name)
+            load(raw, dram_rows, chunk, slice(0, CHUNK_PIX))
             return raw
 
-        def turn(raw_chunks, dram_rows, name, i):
+        def turn(raw_chunks, dram_rows, name, i, h):
             chunk, part = divmod(i, CHUNK_PASSES)
             words = raw_chunks[chunk][:].bitcast(F32)
-            banks = []
-            for h in range(ROW_TILES * P // BANK_ROWS):
-                bank = turned.tile([P, 2, BANK_ROWS], F32, name="%s_bank%d" % (name, h))
-                for u in range(2):
-                    first = part * PASS_WORDS + u * P
-                    for j in range(BANK_ROWS // P):
-                        nc.tensor.transpose(
-                            bank[:, u, j * P : (j + 1) * P],
-                            words[:, h * (BANK_ROWS // P) + j, first : first + P],
-                            identity[:],
-                        )
-                banks.append(bank)
-            if part == CHUNK_PASSES - 1 and chunk + ROW_BUFS < N_CHUNK:
+            bank = turned.tile([P, 2, BANK_ROWS], F32, name="%s_bank%d" % (name, h))
+            for u in range(2):
+                first = part * PASS_WORDS + u * P
+                for j in range(BANK_ROWS // P):
+                    nc.tensor.transpose(
+                        bank[:, u, j * P : (j + 1) * P],
+                        words[:, h * (BANK_ROWS // P) + j, first : first + P],
+                        identity[:],
+                    )
+            if h == 1 and part == CHUNK_PASSES - 1 and chunk + ROW_BUFS < N_CHUNK:
                 raw_chunks[chunk + ROW_BUFS] = load_chunk(dram_rows, name, chunk + ROW_BUFS)
-            return banks
+            return bank
 
-        def regroup_features(banks, copy, between):
-            grouped = groups.tile([P, C, PACK], BF16, name="f_grouped", align_bytes=64)
-            grouped_words = grouped[:].bitcast(F32)
-            for h, bank in enumerate(banks):
-                copy(
-                    out=grouped_words[:, h * BANK_ROWS : (h + 1) * BANK_ROWS, :],
-                    in_=bank[:].rearrange("p u c -> p c u"),
-                )
-                if h == 0:
-                    between()
-            return grouped
+        def regroup_features(copy, grouped, bank, h):
+            copy(
+                out=grouped[:].bitcast(F32)[:, h * BANK_ROWS : (h + 1) * BANK_ROWS, :],
+                in_=bank[:].rearrange("p u c -> p c u"),
+            )
+
+        def gram(raw_chunks, i):
+            chunk, part = divmod(i, CHUNK_PASSES)
+            first = part * PASS_PIX
+            bank = turned.tile([P, P], F32, name="f_bank1")
+            for r in range(ROW_TILES):
+                pixels = raw_chunks[chunk][:, r, first : first + 2 * P : 2]
+                nc.tensor.matmul(bank[:], lhsT=pixels, rhs=pixels, start=(r == 0), stop=False)
+            nc.tensor.matmul(bank[:], lhsT=identity_bf16[:], rhs=off_diagonal[:], start=False, stop=True)
+            return bank
+
+        def take_diagonal(bank, sumsq):
+            diagonal = scratch.tile([P, P], BF16, name="diagonal")
+            nc.scalar.activation(out=diagonal[:], in_=bank[:], func=ACT.Relu, accum_out=sumsq[:, 0:1])
 
         def sum_squares(grouped, sumsq, slots):
             for t in slots:
                 squares = scratch.tile([P, C], BF16, name="squares")
                 nc.scalar.activation(
                     out=squares[:], in_=grouped[:, :, t], func=ACT.Square, accum_out=sumsq[:, t : t + 1]
+                )
+
+        def sum_squares_on_vector(grouped, sumsq, slots):
+            for t in slots:
+                squares = scratch.tile([P, C], BF16, name="squares_v")
+                nc.vector.scalar_tensor_tensor(
+                    out=squares[:],
+                    in0=grouped[:, :, t],
+                    scalar=1.0,
+                    in1=grouped[:, :, t],
+                    op0=ALU.mult,
+                    op1=ALU.mult,
+                    accum_out=sumsq[:, t : t + 1],
                 )
 
         def roots(sumsq):
@@ -114,25 +148,43 @@ def tile_globalprototype_kernel(tc, features, prototypes, grad_out, out):
             nc.vector.reciprocal(out=inv_norm[:], in_=norm[:])
             return inv_norm
 
-        def scale_gradients(banks, inv_norm):
-            gs = groups.tile([P, K, PACK], BF16, name="gs", align_bytes=64)
-            per_pixel = inv_norm[:].rearrange("p (u e) -> p u e", u=2).unsqueeze(1)
-            for h, bank in enumerate(banks):
-                nc.vector.tensor_tensor(
-                    out=gs[:, h * BANK_ROWS : (h + 1) * BANK_ROWS, :].rearrange("p k (u e) -> p k u e", u=2),
-                    in0=bank[:].bitcast(BF16).rearrange("p u (k e) -> p k u e", e=2),
-                    in1=per_pixel.to_broadcast([P, BANK_ROWS, 2, 2]),
-                    op=ALU.mult,
-                )
-            return gs
+        def regroup_share(bank):
+            share = groups.tile([P, SHARE_ROWS, PACK], BF16, name="share", align_bytes=64)
+            nc.scalar.copy(
+                out=share[:].bitcast(F32), in_=bank[:, :, BANK_ROWS - SHARE_ROWS :].rearrange("p u k -> p k u")
+            )
+            return share
 
-        def quantise(grouped, width, fmt, name):
+        def scale_share(gs, share, inv_norm):
+            nc.gpsimd.tensor_tensor(
+                out=gs[:, BANK_ROWS - SHARE_ROWS : BANK_ROWS, :],
+                in0=share[:],
+                in1=inv_norm[:].unsqueeze(1).to_broadcast([P, SHARE_ROWS, PACK]),
+                op=ALU.mult,
+            )
+
+        def scale_gradients(gs, bank, inv_norm, h):
+            count = BANK_ROWS - SHARE_ROWS if h == 0 else BANK_ROWS
+            per_pixel = inv_norm[:].rearrange("p (u e) -> p u e", u=2).unsqueeze(1)
+            nc.vector.tensor_tensor(
+                out=gs[:, h * BANK_ROWS : h * BANK_ROWS + count, :].rearrange("p k (u e) -> p k u e", u=2),
+                in0=bank[:].bitcast(BF16).rearrange("p u (k e) -> p k u e", e=2)[:, :count],
+                in1=per_pixel.to_broadcast([P, count, 2, 2]),
+                op=ALU.mult,
+            )
+
+        def new_mx(width, name):
             codes = packed.tile([P, width], U32, name=name + "_codes", align_bytes=64)
             scales = packed.tile([P, width], U8, name=name + "_scales", align_bytes=64)
-            nc.vector.quantize_mx(
-                out=codes[:].bitcast(fmt), scales=scales[:], in_=grouped[:].rearrange("p w t -> p (w t)")
-            )
             return codes, scales
+
+        def quantise(mx, grouped, fmt, cols):
+            codes, scales = mx
+            nc.vector.quantize_mx(
+                out=codes[:, cols].bitcast(fmt),
+                scales=scales[:, cols],
+                in_=grouped[:, cols, :].rearrange("p w t -> p (w t)"),
+            )
 
         def multiply(i, g_mx, f_mx, row_tiles):
             g_codes, g_scales = g_mx
@@ -150,7 +202,12 @@ def tile_globalprototype_kernel(tc, features, prototypes, grad_out, out):
                 )
 
         f_raw, g_raw = {}, {}
-        for chunk in range(ROW_BUFS):
+        f_raw[0], g_raw[0] = new_chunk("f"), new_chunk("g")
+        for part in range(CHUNK_PASSES):
+            pixels = slice(part * PASS_PIX, (part + 1) * PASS_PIX)
+            load(f_raw[0], f_rows, 0, pixels)
+            load(g_raw[0], g_rows, 0, pixels)
+        for chunk in range(1, ROW_BUFS):
             f_raw[chunk] = load_chunk(f_rows, "f", chunk)
             g_raw[chunk] = load_chunk(g_rows, "g", chunk)
         protos = const.tile([P, ROW_TILES, C], BF16, name="protos")
@@ -159,39 +216,102 @@ def tile_globalprototype_kernel(tc, features, prototypes, grad_out, out):
         def is_pass(j):
             return 0 <= j < N_PASS
 
-        f_banks, g_banks, f_grouped, sumsq, norm, inv_norm, gs, f_mx, g_mx = {}, {}, {}, {}, {}, {}, {}, {}, {}
+        last = N_PASS - 1
+        f_banks, g_banks, f_grouped, share, sumsq, norm, inv_norm, gs, f_mx, g_mx = [{} for n in range(10)]
+
+        def turn_features(j, h):
+            f_banks[j, h] = turn(f_raw, f_rows, "f", j, h)
+
+        def turn_gradients(j, h):
+            g_banks[j, h] = turn(g_raw, g_rows, "g", j, h)
+
+        def empty_features(j, h, copy):
+            regroup_features(copy, f_grouped[j], f_banks[j, h], h)
+
+        def new_features(j):
+            f_grouped[j] = groups.tile([P, C, PACK], BF16, name="f_grouped", align_bytes=64)
+            sumsq[j] = small.tile([P, PACK], F32, name="sumsq")
 
         def take_roots(j):
-            if is_pass(j):
-                norm[j] = roots(sumsq[j])
+            norm[j] = roots(sumsq[j])
 
-        for i in range(-4, N_PASS + 1):
-            if is_pass(i):
-                gs[i] = scale_gradients(g_banks[i], inv_norm[i])
-            if is_pass(i + 3):
-                f_grouped[i + 3] = regroup_features(
-                    f_banks[i + 3],
-                    nc.vector.tensor_copy if i + 3 < VECTOR_COPIES else nc.scalar.copy,
-                    lambda: take_roots(i + 1),
-                )
-            else:
-                take_roots(i + 1)
-            if is_pass(i + 1):
-                inv_norm[i + 1] = inverse_norms(norm[i + 1])
+        def quantise_features(j):
+            f_mx[j] = new_mx(C, "f")
+            quantise(f_mx[j], f_grouped[j], E4M3_X4, slice(0, C))
+
+        turn_features(0, 0)
+        turn_features(0, 1)
+        new_features(0)
+        empty_features(0, 0, nc.scalar.copy)
+        empty_features(0, 1, nc.vector.tensor_copy)
+        sum_squares(f_grouped[0], sumsq[0], (0, 1))
+        sum_squares_on_vector(f_grouped[0], sumsq[0], (2, 3))
+        turn_features(1, 0)
+        turn_features(1, 1)
+        turn_gradients(0, 0)
+        turn_gradients(0, 1)
+        take_roots(0)
+        new_features(1)
+        empty_features(1, 0, nc.scalar.copy)
+        empty_features(1, 1, nc.vector.tensor_copy)
+        share[0] = regroup_share(g_banks[0, 0])
+        f_gram = gram(f_raw, 1)
+        turn_features(2, 0)
+        quantise_features(0)
+        inv_norm[0] = inverse_norms(norm[0])
+        sum_squares(f_grouped[1], sumsq[1], (1, 2))
+        take_diagonal(f_gram, sumsq[1])
+        sum_squares(f_grouped[1], sumsq[1], (3,))
+        turn_features(2, 1)
+        quantise_features(1)
+        new_features(2)
+        empty_features(2, 0, nc.scalar.copy)
+        take_roots(1)
+        empty_features(2, 1, nc.scalar.copy)
+        turn_features(3, 0)
+        turn_features(3, 1)
+
+        for i in range(N_PASS):
+            gs[i] = groups.tile([P, K, PACK], BF16, name="gs", align_bytes=64)
+            g_mx[i] = new_mx(K, "g")
+            scale_share(gs[i], share[i], inv_norm[i])
+            scale_gradients(gs[i], g_banks[i, 0], inv_norm[i], 0)
+            if i < last:
+                scale_gradients(gs[i], g_banks[i, 1], inv_norm[i], 1)
             if is_pass(i + 2):
-                sumsq[i + 2] = small.tile([P, PACK], F32, name="sumsq")
-                sum_squares(f_grouped[i + 2], sumsq[i + 2], range(PACK))
-            if is_pass(i - 1):
-                multiply(i - 1, g_mx[i - 1], f_mx[i - 1], (0, 1))
-            if is_pass(i + 1):
-                g_banks[i + 1] = turn(g_raw, g_rows, "g", i + 1)
-                f_mx[i + 1] = quantise(f_grouped[i + 1], C, E4M3_X4, "f")
-            if is_pass(i):
-                g_mx[i] = quantise(gs[i], K, E5M2_X4, "g")
-            if is_pass(i - 1):
+                sum_squares(f_grouped[i + 2], sumsq[i + 2], (1,))
+            if 0 < i < last:
+                take_roots(i + 1)
+            if is_pass(i + 3):
+                new_features(i + 3)
+                empty_features(i + 3, 1, nc.scalar.copy)
+            if i == 0:
+                quantise(g_mx[i], gs[i], E5M2_X4, slice(0, K))
+            if i + 2 < last:
+                quantise_features(i + 2)
+            if i < last:
+                inv_norm[i + 1] = inverse_norms(norm[i + 1])
+                turn_gradients(i + 1, 0)
+                share[i + 1] = regroup_share(g_banks[i + 1, 0])
+            if is_pass(i + 3):
+                empty_features(i + 3, 0, nc.scalar.copy)
+            if 0 < i < last:
+                quantise(g_mx[i], gs[i], E5M2_X4, slice(0, K))
+            if i > 0:
                 multiply(i - 1, g_mx[i - 1], f_mx[i - 1], (2, 3))
+            if i < last:
+                turn_gradients(i + 1, 1)
+            if is_pass(i + 2):
+                f_gram = gram(f_raw, i + 2)
+            if i < last:
+                multiply(i, g_mx[i], f_mx[i], (0, 1))
+            if is_pass(i + 2):
+                sum_squares(f_grouped[i + 2], sumsq[i + 2], (2,))
+                take_diagonal(f_gram, sumsq[i + 2])
+                sum_squares(f_grouped[i + 2], sumsq[i + 2], (3,))
             if is_pass(i + 4):
-                f_banks[i + 4] = turn(f_raw, f_rows, "f", i + 4)
+                turn_features(i + 4, 0)
+                turn_features(i + 4, 1)
 
         p_sumsq = const.tile([P, ROW_TILES], F32, name="p_sumsq")
         p_squares = const.tile([P, ROW_TILES, C], BF16, name="p_squares")
@@ -209,39 +329,55 @@ def tile_globalprototype_kernel(tc, features, prototypes, grad_out, out):
         products = const.tile([P, ROW_TILES, C], F32, name="products")
         m_scaled = const.tile([P, ROW_TILES, C], F32, name="m_scaled")
         result = const.tile([P, ROW_TILES, C], F32, name="result")
-        for step in range(ROW_TILES + 2):
-            r = step
-            if r < ROW_TILES:
-                nc.vector.scalar_tensor_tensor(
-                    out=products[:, r, :],
-                    in0=m_sums[r][:],
-                    scalar=1.0,
-                    in1=protos[:, r, :],
-                    op0=ALU.mult,
-                    op1=ALU.mult,
-                    accum_out=proj[:, r : r + 1],
-                )
-                nc.scalar.activation(
-                    out=m_scaled[:, r, :], in_=m_sums[r][:], func=ACT.Copy, scale=inv_p[:, r : r + 1]
-                )
-            r = step - 1
-            if 0 <= r < ROW_TILES:
-                nc.vector.scalar_tensor_tensor(
-                    out=pull[:, r : r + 1],
-                    in0=proj[:, r : r + 1],
-                    scalar=-1.0,
-                    in1=inv_p3[:, r : r + 1],
-                    op0=ALU.mult,
-                    op1=ALU.mult,
-                )
-            r = step - 2
-            if r >= 0:
-                nc.vector.scalar_tensor_tensor(
-                    out=result[:, r, :],
-                    in0=protos[:, r, :],
-                    scalar=pull[:, r : r + 1],
-                    in1=m_scaled[:, r, :],
-                    op0=ALU.mult,
-                    op1=ALU.add,
-                )
-                nc.sync.dma_start(out=out_rows[r], in_=result[:, r, :])
+
+        def project(r):
+            nc.vector.scalar_tensor_tensor(
+                out=products[:, r, :],
+                in0=m_sums[r][:],
+                scalar=1.0,
+                in1=protos[:, r, :],
+                op0=ALU.mult,
+                op1=ALU.mult,
+                accum_out=proj[:, r : r + 1],
+            )
+            nc.scalar.activation(out=m_scaled[:, r, :], in_=m_sums[r][:], func=ACT.Copy, scale=inv_p[:, r : r + 1])
+
+        def pull_back(r):
+            nc.vector.scalar_tensor_tensor(
+                out=pull[:, r : r + 1],
+                in0=proj[:, r : r + 1],
+                scalar=-1.0,
+                in1=inv_p3[:, r : r + 1],
+                op0=ALU.mult,
+                op1=ALU.mult,
+            )
+
+        def finish(r):
+            nc.vector.scalar_tensor_tensor(
+                out=result[:, r, :],
+                in0=protos[:, r, :],
+                scalar=pull[:, r : r + 1],
+                in1=m_scaled[:, r, :],
+                op0=ALU.mult,
+                op1=ALU.add,
+            )
+            nc.sync.dma_start(out=out_rows[r], in_=result[:, r, :])
+
+        quantise_features(last)
+        quantise(g_mx[last], gs[last], E5M2_X4, slice(0, BANK_ROWS))
+        multiply(last, g_mx[last], f_mx[last], (0, 1))
+        scale_gradients(gs[last], g_banks[last, 1], inv_norm[last], 1)
+        project(0)
+        quantise(g_mx[last], gs[last], E5M2_X4, slice(BANK_ROWS, K))
+        multiply(last, g_mx[last], f_mx[last], (2, 3))
+        pull_back(0)
+        project(1)
+        finish(0)
+        pull_back(1)
+        project(2)
+        project(3)
+        pull_back(2)
+        finish(1)
+        pull_back(3)
+        finish(2)
+        finish(3)

@@ -26,8 +26,7 @@ ROW_BUFS = 5
 BANK_ROWS = 2 * P
 
 
-SHARE_ROWS = 64
-FAR_BELOW = -(2.0**126)
+SHARE_ROWS = 128
 
 FLOPS = 2 * K * C * IMAGES * IMAGE_PIX
 
@@ -54,12 +53,6 @@ def tile_globalprototype_kernel(tc, features, prototypes, grad_out, out):
         nc.scalar.activation(out=warm[:], in_=warm[:], func=ACT.Sqrt)
         identity = const.tile([P, P], F32, name="identity")
         make_identity(nc, identity[:])
-        identity_bf16 = const.tile([P, P], BF16, name="identity_bf16")
-        nc.vector.tensor_copy(out=identity_bf16[:], in_=identity[:])
-        off_diagonal = const.tile([P, P], BF16, name="off_diagonal")
-        nc.vector.tensor_scalar(
-            out=off_diagonal[:], in0=identity[:], scalar1=-FAR_BELOW, scalar2=FAR_BELOW, op0=ALU.mult, op1=ALU.add
-        )
         minus_half = const.tile([P, PACK], F32, name="minus_half")
         nc.gpsimd.memset(minus_half[:], -0.5)
         minus_three_halves = const.tile([P, ROW_TILES], F32, name="minus_three_halves")
@@ -82,7 +75,7 @@ def tile_globalprototype_kernel(tc, features, prototypes, grad_out, out):
             load(raw, dram_rows, chunk, slice(0, CHUNK_PIX))
             return raw
 
-        def turn(raw_chunks, dram_rows, name, i, h):
+        def turn(raw_chunks, name, i, h):
             chunk, part = divmod(i, CHUNK_PASSES)
             words = raw_chunks[chunk][:].bitcast(F32)
             bank = turned.tile([P, 2, BANK_ROWS], F32, name="%s_bank%d" % (name, h))
@@ -94,9 +87,12 @@ def tile_globalprototype_kernel(tc, features, prototypes, grad_out, out):
                         words[:, h * (BANK_ROWS // P) + j, first : first + P],
                         identity[:],
                     )
-            if h == 1 and part == CHUNK_PASSES - 1 and chunk + ROW_BUFS < N_CHUNK:
-                raw_chunks[chunk + ROW_BUFS] = load_chunk(dram_rows, name, chunk + ROW_BUFS)
             return bank
+
+        def refill(raw_chunks, dram_rows, name, i):
+            chunk, part = divmod(i, CHUNK_PASSES)
+            if part == CHUNK_PASSES - 1 and chunk + ROW_BUFS < N_CHUNK:
+                raw_chunks[chunk + ROW_BUFS] = load_chunk(dram_rows, name, chunk + ROW_BUFS)
 
         def regroup_features(copy, grouped, bank, h):
             copy(
@@ -110,13 +106,20 @@ def tile_globalprototype_kernel(tc, features, prototypes, grad_out, out):
             bank = turned.tile([P, P], F32, name="f_bank1")
             for r in range(ROW_TILES):
                 pixels = raw_chunks[chunk][:, r, first : first + 2 * P : 2]
-                nc.tensor.matmul(bank[:], lhsT=pixels, rhs=pixels, start=(r == 0), stop=False)
-            nc.tensor.matmul(bank[:], lhsT=identity_bf16[:], rhs=off_diagonal[:], start=False, stop=True)
+                nc.tensor.matmul(bank[:], lhsT=pixels, rhs=pixels, start=(r == 0), stop=(r == ROW_TILES - 1))
             return bank
 
         def take_diagonal(bank, sumsq):
-            diagonal = scratch.tile([P, P], BF16, name="diagonal")
-            nc.scalar.activation(out=diagonal[:], in_=bank[:], func=ACT.Relu, accum_out=sumsq[:, 0:1])
+            diagonal = scratch.tile([P, P], F32, name="diagonal")
+            nc.vector.scalar_tensor_tensor(
+                out=diagonal[:],
+                in0=bank[:],
+                scalar=1.0,
+                in1=identity[:],
+                op0=ALU.mult,
+                op1=ALU.mult,
+                accum_out=sumsq[:, 0:1],
+            )
 
         def sum_squares(grouped, sumsq, slots):
             for t in slots:
@@ -220,10 +223,10 @@ def tile_globalprototype_kernel(tc, features, prototypes, grad_out, out):
         f_banks, g_banks, f_grouped, share, sumsq, norm, inv_norm, gs, f_mx, g_mx = [{} for n in range(10)]
 
         def turn_features(j, h):
-            f_banks[j, h] = turn(f_raw, f_rows, "f", j, h)
+            f_banks[j, h] = turn(f_raw, "f", j, h)
 
         def turn_gradients(j, h):
-            g_banks[j, h] = turn(g_raw, g_rows, "g", j, h)
+            g_banks[j, h] = turn(g_raw, "g", j, h)
 
         def empty_features(j, h, copy):
             regroup_features(copy, f_grouped[j], f_banks[j, h], h)
@@ -248,6 +251,7 @@ def tile_globalprototype_kernel(tc, features, prototypes, grad_out, out):
         sum_squares_on_vector(f_grouped[0], sumsq[0], (2, 3))
         turn_features(1, 0)
         turn_features(1, 1)
+        refill(f_raw, f_rows, "f", 1)
         turn_gradients(0, 0)
         turn_gradients(0, 1)
         take_roots(0)
@@ -259,17 +263,17 @@ def tile_globalprototype_kernel(tc, features, prototypes, grad_out, out):
         turn_features(2, 0)
         quantise_features(0)
         inv_norm[0] = inverse_norms(norm[0])
-        sum_squares(f_grouped[1], sumsq[1], (1, 2))
         take_diagonal(f_gram, sumsq[1])
-        sum_squares(f_grouped[1], sumsq[1], (3,))
+        sum_squares(f_grouped[1], sumsq[1], (1, 2, 3))
         turn_features(2, 1)
         quantise_features(1)
         new_features(2)
         empty_features(2, 0, nc.scalar.copy)
         take_roots(1)
         empty_features(2, 1, nc.scalar.copy)
-        turn_features(3, 0)
         turn_features(3, 1)
+        turn_features(3, 0)
+        refill(f_raw, f_rows, "f", 3)
 
         for i in range(N_PASS):
             gs[i] = groups.tile([P, K, PACK], BF16, name="gs", align_bytes=64)
@@ -280,11 +284,11 @@ def tile_globalprototype_kernel(tc, features, prototypes, grad_out, out):
                 scale_gradients(gs[i], g_banks[i, 1], inv_norm[i], 1)
             if is_pass(i + 2):
                 sum_squares(f_grouped[i + 2], sumsq[i + 2], (1,))
-            if 0 < i < last:
-                take_roots(i + 1)
             if is_pass(i + 3):
                 new_features(i + 3)
                 empty_features(i + 3, 1, nc.scalar.copy)
+            if 0 < i < last:
+                take_roots(i + 1)
             if i == 0:
                 quantise(g_mx[i], gs[i], E5M2_X4, slice(0, K))
             if i + 2 < last:
@@ -292,26 +296,27 @@ def tile_globalprototype_kernel(tc, features, prototypes, grad_out, out):
             if i < last:
                 inv_norm[i + 1] = inverse_norms(norm[i + 1])
                 turn_gradients(i + 1, 0)
-                share[i + 1] = regroup_share(g_banks[i + 1, 0])
             if is_pass(i + 3):
                 empty_features(i + 3, 0, nc.scalar.copy)
             if 0 < i < last:
                 quantise(g_mx[i], gs[i], E5M2_X4, slice(0, K))
             if i > 0:
                 multiply(i - 1, g_mx[i - 1], f_mx[i - 1], (2, 3))
-            if i < last:
-                turn_gradients(i + 1, 1)
             if is_pass(i + 2):
                 f_gram = gram(f_raw, i + 2)
             if i < last:
-                multiply(i, g_mx[i], f_mx[i], (0, 1))
+                turn_gradients(i + 1, 1)
+                refill(g_raw, g_rows, "g", i + 1)
+                share[i + 1] = regroup_share(g_banks[i + 1, 0])
+            if i > 0:
+                multiply(i - 1, g_mx[i - 1], f_mx[i - 1], (0, 1))
             if is_pass(i + 2):
-                sum_squares(f_grouped[i + 2], sumsq[i + 2], (2,))
                 take_diagonal(f_gram, sumsq[i + 2])
-                sum_squares(f_grouped[i + 2], sumsq[i + 2], (3,))
+                sum_squares(f_grouped[i + 2], sumsq[i + 2], (2, 3))
             if is_pass(i + 4):
-                turn_features(i + 4, 0)
                 turn_features(i + 4, 1)
+                turn_features(i + 4, 0)
+                refill(f_raw, f_rows, "f", i + 4)
 
         p_sumsq = const.tile([P, ROW_TILES], F32, name="p_sumsq")
         p_squares = const.tile([P, ROW_TILES, C], BF16, name="p_squares")

@@ -27,6 +27,7 @@ BANK_ROWS = 2 * P
 
 
 SHARE_ROWS = 128
+EASE_COLS = 64
 
 FLOPS = 2 * K * C * IMAGES * IMAGE_PIX
 
@@ -75,10 +76,18 @@ def tile_globalprototype_kernel(tc, features, prototypes, grad_out, out):
             load(raw, dram_rows, chunk, slice(0, CHUNK_PIX))
             return raw
 
-        def turn(raw_chunks, name, i, h):
+        def ease_change(raw_chunks, name, i, h):
+            chunk, part = divmod(i, CHUNK_PASSES)
+            values = raw_chunks[chunk][:, 0, part * PASS_PIX : (part + 1) * PASS_PIX]
+            bank = turned.tile([P, 2, BANK_ROWS], F32, name="%s_bank%d" % (name, h))
+            nc.tensor.matmul(bank[:, 0, :EASE_COLS], lhsT=values[:, :P], rhs=values[:, :EASE_COLS], start=True, stop=True)
+            return bank
+
+        def turn(raw_chunks, name, i, h, bank=None):
             chunk, part = divmod(i, CHUNK_PASSES)
             words = raw_chunks[chunk][:].bitcast(F32)
-            bank = turned.tile([P, 2, BANK_ROWS], F32, name="%s_bank%d" % (name, h))
+            if bank is None:
+                bank = turned.tile([P, 2, BANK_ROWS], F32, name="%s_bank%d" % (name, h))
             for u in range(2):
                 first = part * PASS_WORDS + u * P
                 for j in range(BANK_ROWS // P):
@@ -222,8 +231,8 @@ def tile_globalprototype_kernel(tc, features, prototypes, grad_out, out):
         last = N_PASS - 1
         f_banks, g_banks, f_grouped, share, sumsq, norm, inv_norm, gs, f_mx, g_mx = [{} for n in range(10)]
 
-        def turn_features(j, h):
-            f_banks[j, h] = turn(f_raw, "f", j, h)
+        def turn_features(j, h, bank=None):
+            f_banks[j, h] = turn(f_raw, "f", j, h, bank)
 
         def turn_gradients(j, h):
             g_banks[j, h] = turn(g_raw, "g", j, h)
@@ -314,7 +323,7 @@ def tile_globalprototype_kernel(tc, features, prototypes, grad_out, out):
                 take_diagonal(f_gram, sumsq[i + 2])
                 sum_squares(f_grouped[i + 2], sumsq[i + 2], (2, 3))
             if is_pass(i + 4):
-                turn_features(i + 4, 1)
+                turn_features(i + 4, 1, ease_change(f_raw, "f", i + 4, 1))
                 turn_features(i + 4, 0)
                 refill(f_raw, f_rows, "f", i + 4)
 

@@ -29,13 +29,18 @@ BANK_ROWS = 2 * P
 SHARE_ROWS = 128
 EASE_COLS = 64
 
+
+def gram_places(i):
+    return {0: 3, 1: 2}.get(i, 1)
+
+
 FLOPS = 2 * K * C * IMAGES * IMAGE_PIX
 
 
 def tile_globalprototype_kernel(tc, features, prototypes, grad_out, out):
     nc = tc.nc
-    f_rows = features.rearrange("b (r p) h w -> b r p (h w)", p=P)
-    g_rows = grad_out.rearrange("b (r p) h w -> b r p (h w)", p=P)
+    f_rows = features.rearrange("b (r p) h w -> b p r (h w)", p=P)
+    g_rows = grad_out.rearrange("b (r p) h w -> b p r (h w)", p=P)
     out_rows = out.rearrange("(r p) c -> r p c", p=P)
 
     with ExitStack() as ctx:
@@ -54,26 +59,26 @@ def tile_globalprototype_kernel(tc, features, prototypes, grad_out, out):
         nc.scalar.activation(out=warm[:], in_=warm[:], func=ACT.Sqrt)
         identity = const.tile([P, P], F32, name="identity")
         make_identity(nc, identity[:])
-        minus_half = const.tile([P, PACK], F32, name="minus_half")
-        nc.gpsimd.memset(minus_half[:], -0.5)
-        minus_three_halves = const.tile([P, ROW_TILES], F32, name="minus_three_halves")
-        nc.gpsimd.memset(minus_three_halves[:], -1.5)
 
         m_sums = [sums.tile([P, C], F32, name="m_sum%d" % r) for r in range(ROW_TILES)]
 
         def new_chunk(name):
             return rows.tile([P, ROW_TILES, CHUNK_PIX], BF16, name=name)
 
-        def load(raw, dram_rows, chunk, pixels):
+        def load(raw, dram_rows, chunk, row_tiles, pixels):
             image, first = divmod(chunk * CHUNK_PIX, IMAGE_PIX)
-            for r in range(ROW_TILES):
-                nc.sync.dma_start(
-                    out=raw[:, r, pixels], in_=dram_rows[image, r, :, first + pixels.start : first + pixels.stop]
-                )
+            nc.sync.dma_start(
+                out=raw[:, row_tiles, pixels],
+                in_=dram_rows[image, :, row_tiles, first + pixels.start : first + pixels.stop],
+            )
+
+        def load_pass(raw, dram_rows, i, row_tiles=slice(0, ROW_TILES)):
+            chunk, part = divmod(i, CHUNK_PASSES)
+            load(raw, dram_rows, chunk, row_tiles, slice(part * PASS_PIX, (part + 1) * PASS_PIX))
 
         def load_chunk(dram_rows, name, chunk):
             raw = new_chunk(name)
-            load(raw, dram_rows, chunk, slice(0, CHUNK_PIX))
+            load(raw, dram_rows, chunk, slice(0, ROW_TILES), slice(0, CHUNK_PIX))
             return raw
 
         def ease_change(raw_chunks, name, i, h):
@@ -109,25 +114,41 @@ def tile_globalprototype_kernel(tc, features, prototypes, grad_out, out):
                 in_=bank[:].rearrange("p u c -> p c u"),
             )
 
-        def gram(raw_chunks, i):
+        def inner_products(bank, i, t):
             chunk, part = divmod(i, CHUNK_PASSES)
-            first = part * PASS_PIX
-            bank = turned.tile([P, P], F32, name="f_bank1")
+            first = part * PASS_PIX + (t // 2) * 2 * P + t % 2
             for r in range(ROW_TILES):
-                pixels = raw_chunks[chunk][:, r, first : first + 2 * P : 2]
-                nc.tensor.matmul(bank[:], lhsT=pixels, rhs=pixels, start=(r == 0), stop=(r == ROW_TILES - 1))
+                pixels = f_raw[chunk][:, r, first : first + 2 * P - 1 : 2]
+                nc.tensor.matmul(bank, lhsT=pixels, rhs=pixels, start=(r == 0), stop=(r == ROW_TILES - 1))
+
+        def gram(i):
+            bank = turned.tile([P, gram_places(i), P], F32, name="f_bank1")
+            for t in range(gram_places(i)):
+                inner_products(bank[:, t, :], i, t)
             return bank
 
-        def take_diagonal(bank, sumsq):
+        def take_diagonals(bank, i):
+            for t in range(gram_places(i)):
+                take_diagonal(bank[:, t, :], sumsq[i], t)
+
+        def head_gram(i):
+            for t in range(gram_places(i)):
+                inner_products(m_sums[(2 * i + t + i) % ROW_TILES][:, :P], i, t)
+
+        def head_diagonals(i):
+            for t in range(gram_places(i)):
+                take_diagonal(m_sums[(2 * i + t + i) % ROW_TILES][:, :P], sumsq[i], t)
+
+        def take_diagonal(bank, sumsq, t=0):
             diagonal = scratch.tile([P, P], F32, name="diagonal")
             nc.vector.scalar_tensor_tensor(
                 out=diagonal[:],
-                in0=bank[:],
+                in0=bank,
                 scalar=1.0,
                 in1=identity[:],
                 op0=ALU.mult,
                 op1=ALU.mult,
-                accum_out=sumsq[:, 0:1],
+                accum_out=sumsq[:, t : t + 1],
             )
 
         def sum_squares(grouped, sumsq, slots):
@@ -214,12 +235,17 @@ def tile_globalprototype_kernel(tc, features, prototypes, grad_out, out):
                 )
 
         f_raw, g_raw = {}, {}
-        f_raw[0], g_raw[0] = new_chunk("f"), new_chunk("g")
-        for part in range(CHUNK_PASSES):
-            pixels = slice(part * PASS_PIX, (part + 1) * PASS_PIX)
-            load(f_raw[0], f_rows, 0, pixels)
-            load(g_raw[0], g_rows, 0, pixels)
-        for chunk in range(1, ROW_BUFS):
+        for chunk in range(2):
+            f_raw[chunk], g_raw[chunk] = new_chunk("f"), new_chunk("g")
+        load_pass(f_raw[0], f_rows, 0, slice(0, 2))
+        load_pass(f_raw[0], f_rows, 0, slice(2, 4))
+        load_pass(f_raw[0], f_rows, 1)
+        load_pass(g_raw[0], g_rows, 0)
+        load_pass(f_raw[1], f_rows, 2)
+        load_pass(g_raw[0], g_rows, 1)
+        load_pass(f_raw[1], f_rows, 3)
+        load(g_raw[1], g_rows, 1, slice(0, ROW_TILES), slice(0, CHUNK_PIX))
+        for chunk in range(2, ROW_BUFS):
             f_raw[chunk] = load_chunk(f_rows, "f", chunk)
             g_raw[chunk] = load_chunk(g_rows, "g", chunk)
         protos = const.tile([P, ROW_TILES, C], BF16, name="protos")
@@ -254,65 +280,58 @@ def tile_globalprototype_kernel(tc, features, prototypes, grad_out, out):
         turn_features(0, 0)
         turn_features(0, 1)
         new_features(0)
+        new_features(1)
         empty_features(0, 0, nc.scalar.copy)
         empty_features(0, 1, nc.vector.tensor_copy)
-        sum_squares(f_grouped[0], sumsq[0], (0, 1))
-        sum_squares_on_vector(f_grouped[0], sumsq[0], (2, 3))
+        head_gram(0)
+        head_diagonals(0)
+        sum_squares(f_grouped[0], sumsq[0], range(gram_places(0), PACK))
         turn_features(1, 0)
         turn_features(1, 1)
         refill(f_raw, f_rows, "f", 1)
+        head_gram(1)
         turn_gradients(0, 0)
         turn_gradients(0, 1)
-        take_roots(0)
-        new_features(1)
-        empty_features(1, 0, nc.scalar.copy)
-        empty_features(1, 1, nc.vector.tensor_copy)
-        share[0] = regroup_share(g_banks[0, 0])
-        f_gram = gram(f_raw, 1)
-        turn_features(2, 0)
         quantise_features(0)
+        empty_features(1, 0, nc.scalar.copy)
+        take_roots(0)
+        empty_features(1, 1, nc.scalar.copy)
         inv_norm[0] = inverse_norms(norm[0])
-        take_diagonal(f_gram, sumsq[1])
-        sum_squares(f_grouped[1], sumsq[1], (1, 2, 3))
+        head_diagonals(1)
+        share[0] = regroup_share(g_banks[0, 0])
+        sum_squares(f_grouped[1], sumsq[1], (2, 3))
         turn_features(2, 1)
-        quantise_features(1)
-        new_features(2)
-        empty_features(2, 0, nc.scalar.copy)
-        take_roots(1)
-        empty_features(2, 1, nc.scalar.copy)
-        turn_features(3, 1)
-        turn_features(3, 0)
-        refill(f_raw, f_rows, "f", 3)
+        turn_features(2, 0)
 
         for i in range(N_PASS):
             gs[i] = groups.tile([P, K, PACK], BF16, name="gs", align_bytes=64)
             g_mx[i] = new_mx(K, "g")
             scale_share(gs[i], share[i], inv_norm[i])
-            scale_gradients(gs[i], g_banks[i, 0], inv_norm[i], 0)
             if i < last:
-                scale_gradients(gs[i], g_banks[i, 1], inv_norm[i], 1)
+                scale_gradients(gs[i], g_banks[i, 0], inv_norm[i], 0)
+            else:
+                quantise_features(i)
+            scale_gradients(gs[i], g_banks[i, 1], inv_norm[i], 1)
+            if is_pass(i + 1):
+                sum_squares(f_grouped[i + 1], sumsq[i + 1], range(gram_places(i + 1), 2))
             if is_pass(i + 2):
-                sum_squares(f_grouped[i + 2], sumsq[i + 2], (1,))
-            if is_pass(i + 3):
-                new_features(i + 3)
-                empty_features(i + 3, 1, nc.scalar.copy)
-            if 0 < i < last:
+                new_features(i + 2)
+                empty_features(i + 2, 1, nc.scalar.copy)
+            if i < last:
                 take_roots(i + 1)
-            if i == 0:
-                quantise(g_mx[i], gs[i], E5M2_X4, slice(0, K))
-            if i + 2 < last:
-                quantise_features(i + 2)
+            if i + 1 < last:
+                quantise_features(i + 1)
             if i < last:
                 inv_norm[i + 1] = inverse_norms(norm[i + 1])
                 turn_gradients(i + 1, 0)
-            if is_pass(i + 3):
-                empty_features(i + 3, 0, nc.scalar.copy)
-            if 0 < i < last:
+            if is_pass(i + 2):
+                empty_features(i + 2, 0, nc.scalar.copy)
+            if i < last:
                 quantise(g_mx[i], gs[i], E5M2_X4, slice(0, K))
             if i > 0:
                 multiply(i - 1, g_mx[i - 1], f_mx[i - 1], (2, 3))
             if is_pass(i + 2):
-                f_gram = gram(f_raw, i + 2)
+                f_gram = gram(i + 2)
             if i < last:
                 turn_gradients(i + 1, 1)
                 refill(g_raw, g_rows, "g", i + 1)
@@ -320,12 +339,12 @@ def tile_globalprototype_kernel(tc, features, prototypes, grad_out, out):
             if i > 0:
                 multiply(i - 1, g_mx[i - 1], f_mx[i - 1], (0, 1))
             if is_pass(i + 2):
-                take_diagonal(f_gram, sumsq[i + 2])
+                take_diagonals(f_gram, i + 2)
                 sum_squares(f_grouped[i + 2], sumsq[i + 2], (2, 3))
-            if is_pass(i + 4):
-                turn_features(i + 4, 1, ease_change(f_raw, "f", i + 4, 1))
-                turn_features(i + 4, 0)
-                refill(f_raw, f_rows, "f", i + 4)
+            if is_pass(i + 3):
+                turn_features(i + 3, 1, ease_change(f_raw, "f", i + 3, 1))
+                turn_features(i + 3, 0)
+                refill(f_raw, f_rows, "f", i + 3)
 
         p_sumsq = const.tile([P, ROW_TILES], F32, name="p_sumsq")
         p_squares = const.tile([P, ROW_TILES, C], BF16, name="p_squares")
@@ -333,10 +352,11 @@ def tile_globalprototype_kernel(tc, features, prototypes, grad_out, out):
             nc.scalar.activation(
                 out=p_squares[:, r, :], in_=protos[:, r, :], func=ACT.Square, accum_out=p_sumsq[:, r : r + 1]
             )
+        p_norm = const.tile([P, ROW_TILES], F32, name="p_norm")
+        nc.scalar.activation(out=p_norm[:], in_=p_sumsq[:], func=ACT.Sqrt)
         inv_p = const.tile([P, ROW_TILES], F32, name="inv_p")
-        nc.gpsimd.tensor_tensor(out=inv_p[:], in0=p_sumsq[:], in1=minus_half[:], op=ALU.pow)
+        inv_p2 = const.tile([P, ROW_TILES], F32, name="inv_p2")
         inv_p3 = const.tile([P, ROW_TILES], F32, name="inv_p3")
-        nc.gpsimd.tensor_tensor(out=inv_p3[:], in0=p_sumsq[:], in1=minus_three_halves[:], op=ALU.pow)
 
         proj = const.tile([P, ROW_TILES], F32, name="proj")
         pull = const.tile([P, ROW_TILES], F32, name="pull")
@@ -377,21 +397,23 @@ def tile_globalprototype_kernel(tc, features, prototypes, grad_out, out):
             )
             nc.sync.dma_start(out=out_rows[r], in_=result[:, r, :])
 
-        quantise_features(last)
-        quantise(g_mx[last], gs[last], E5M2_X4, slice(0, BANK_ROWS))
-        multiply(last, g_mx[last], f_mx[last], (0, 1))
-        scale_gradients(gs[last], g_banks[last, 1], inv_norm[last], 1)
-        project(0)
         quantise(g_mx[last], gs[last], E5M2_X4, slice(BANK_ROWS, K))
         multiply(last, g_mx[last], f_mx[last], (2, 3))
-        pull_back(0)
-        project(1)
-        finish(0)
-        pull_back(1)
+        scale_gradients(gs[last], g_banks[last, 0], inv_norm[last], 0)
+        nc.vector.reciprocal(out=inv_p[:], in_=p_norm[:])
+        nc.gpsimd.tensor_tensor(out=inv_p2[:], in0=inv_p[:], in1=inv_p[:], op=ALU.mult)
+        nc.gpsimd.tensor_tensor(out=inv_p3[:], in0=inv_p2[:], in1=inv_p[:], op=ALU.mult)
+        quantise(g_mx[last], gs[last], E5M2_X4, slice(0, BANK_ROWS))
+        multiply(last, g_mx[last], f_mx[last], (0, 1))
         project(2)
         project(3)
         pull_back(2)
-        finish(1)
+        project(0)
         pull_back(3)
         finish(2)
+        project(1)
+        pull_back(0)
         finish(3)
+        pull_back(1)
+        finish(0)
+        finish(1)

@@ -26,7 +26,7 @@ ROW_BUFS = 5
 BANK_ROWS = 2 * P
 
 
-SHARE_ROWS = 128
+SHARE_ROWS = 160
 EASE_COLS = 64
 
 

@@ -26,12 +26,12 @@ ROW_BUFS = 5
 BANK_ROWS = 2 * P
 
 
-SHARE_ROWS = 160
-EASE_COLS = 64
+SHARE_ROWS = 192
+EASE_COLS = 16
 
 
 def gram_places(i):
-    return {0: 3, 1: 2}.get(i, 1)
+    return {0: 3, 1: 2}.get(i, 1 + i % 2)
 
 
 FLOPS = 2 * K * C * IMAGES * IMAGE_PIX

@@ -28,10 +28,14 @@ BANK_ROWS = 2 * P
 
 SHARE_ROWS = 192
 EASE_COLS = 16
+WAIT_BANK = 2
+FIRST_DOUBLE = 9
 
 
 def gram_places(i):
-    return {0: 3, 1: 2}.get(i, 1 + i % 2)
+    if i < 2:
+        return 3 - i
+    return 2 if i % 2 and i >= FIRST_DOUBLE else 1
 
 
 FLOPS = 2 * K * C * IMAGES * IMAGE_PIX
@@ -57,10 +61,16 @@ def tile_globalprototype_kernel(tc, features, prototypes, grad_out, out):
         warm = const.tile([P, 1], F32, name="warm")
         nc.vector.memset(warm[:], 1.0)
         nc.scalar.activation(out=warm[:], in_=warm[:], func=ACT.Sqrt)
+        zeros = const.tile([P, P], F32, name="zeros")
+        nc.vector.memset(zeros[:], 0.0)
         identity = const.tile([P, P], F32, name="identity")
         make_identity(nc, identity[:])
 
         m_sums = [sums.tile([P, C], F32, name="m_sum%d" % r) for r in range(ROW_TILES)]
+
+        def keep_clock(count):
+            for n in range(count):
+                nc.tensor.matmul(m_sums[WAIT_BANK][:, P : 2 * P], lhsT=zeros[:], rhs=zeros[:], start=True, stop=True)
 
         def new_chunk(name):
             return rows.tile([P, ROW_TILES, CHUNK_PIX], BF16, name=name)
@@ -133,11 +143,11 @@ def tile_globalprototype_kernel(tc, features, prototypes, grad_out, out):
 
         def head_gram(i):
             for t in range(gram_places(i)):
-                inner_products(m_sums[(2 * i + t + i) % ROW_TILES][:, :P], i, t)
+                inner_products(m_sums[(3 * i + t) % ROW_TILES][:, :P], i, t)
 
         def head_diagonals(i):
             for t in range(gram_places(i)):
-                take_diagonal(m_sums[(2 * i + t + i) % ROW_TILES][:, :P], sumsq[i], t)
+                take_diagonal(m_sums[(3 * i + t) % ROW_TILES][:, :P], sumsq[i], t)
 
         def take_diagonal(bank, sumsq, t=0):
             diagonal = scratch.tile([P, P], F32, name="diagonal")
@@ -277,6 +287,7 @@ def tile_globalprototype_kernel(tc, features, prototypes, grad_out, out):
             f_mx[j] = new_mx(C, "f")
             quantise(f_mx[j], f_grouped[j], E4M3_X4, slice(0, C))
 
+        keep_clock(4)
         turn_features(0, 0)
         turn_features(0, 1)
         new_features(0)
@@ -292,6 +303,7 @@ def tile_globalprototype_kernel(tc, features, prototypes, grad_out, out):
         head_gram(1)
         turn_gradients(0, 0)
         turn_gradients(0, 1)
+        keep_clock(2)
         quantise_features(0)
         empty_features(1, 0, nc.scalar.copy)
         take_roots(0)
@@ -302,16 +314,19 @@ def tile_globalprototype_kernel(tc, features, prototypes, grad_out, out):
         sum_squares(f_grouped[1], sumsq[1], (2, 3))
         turn_features(2, 1)
         turn_features(2, 0)
+        keep_clock(2)
 
         for i in range(N_PASS):
             gs[i] = groups.tile([P, K, PACK], BF16, name="gs", align_bytes=64)
             g_mx[i] = new_mx(K, "g")
             scale_share(gs[i], share[i], inv_norm[i])
-            if i < last:
+            if 0 < i < last:
                 scale_gradients(gs[i], g_banks[i, 0], inv_norm[i], 0)
-            else:
+            if i == last:
                 quantise_features(i)
             scale_gradients(gs[i], g_banks[i, 1], inv_norm[i], 1)
+            if i == 0:
+                scale_gradients(gs[i], g_banks[i, 0], inv_norm[i], 0)
             if is_pass(i + 1):
                 sum_squares(f_grouped[i + 1], sumsq[i + 1], range(gram_places(i + 1), 2))
             if is_pass(i + 2):
@@ -338,6 +353,8 @@ def tile_globalprototype_kernel(tc, features, prototypes, grad_out, out):
                 share[i + 1] = regroup_share(g_banks[i + 1, 0])
             if i > 0:
                 multiply(i - 1, g_mx[i - 1], f_mx[i - 1], (0, 1))
+            else:
+                keep_clock(3)
             if is_pass(i + 2):
                 take_diagonals(f_gram, i + 2)
                 sum_squares(f_grouped[i + 2], sumsq[i + 2], (2, 3))

@@ -22,6 +22,7 @@ N_PASS = IMAGES * IMAGE_PIX // PASS_PIX
 CHUNK_PASSES = 2
 CHUNK_PIX = CHUNK_PASSES * PASS_PIX
 N_CHUNK = N_PASS // CHUNK_PASSES
+FIRST_CHUNK = 2
 ROW_BUFS = 5
 BANK_ROWS = 2 * P
 
@@ -72,51 +73,49 @@ def tile_globalprototype_kernel(tc, features, prototypes, grad_out, out):
             for n in range(count):
                 nc.tensor.matmul(m_sums[WAIT_BANK][:, P : 2 * P], lhsT=zeros[:], rhs=zeros[:], start=True, stop=True)
 
-        def new_chunk(name):
-            return rows.tile([P, ROW_TILES, CHUNK_PIX], BF16, name=name)
 
-        def load(raw, dram_rows, chunk, row_tiles, pixels):
-            image, first = divmod(chunk * CHUNK_PIX, IMAGE_PIX)
-            nc.sync.dma_start(
-                out=raw[:, row_tiles, pixels],
-                in_=dram_rows[image, :, row_tiles, first + pixels.start : first + pixels.stop],
-            )
+        f_raw, g_raw = {}, {}
 
-        def load_pass(raw, dram_rows, i, row_tiles=slice(0, ROW_TILES)):
-            chunk, part = divmod(i, CHUNK_PASSES)
-            load(raw, dram_rows, chunk, row_tiles, slice(part * PASS_PIX, (part + 1) * PASS_PIX))
+        def load(out, dram_rows, i, row_tiles=slice(0, ROW_TILES)):
+            image, first = divmod(i * PASS_PIX, IMAGE_PIX)
+            nc.sync.dma_start(out=out, in_=dram_rows[image, :, row_tiles, first : first + out.shape[2]])
 
-        def load_chunk(dram_rows, name, chunk):
-            raw = new_chunk(name)
-            load(raw, dram_rows, chunk, slice(0, ROW_TILES), slice(0, CHUNK_PIX))
-            return raw
+        def new_pass(raw, name, i):
+            raw[i] = rows.tile([P, ROW_TILES, PASS_PIX], BF16, name="%s_pass%d" % (name, i), bufs=1)[:]
 
-        def ease_change(raw_chunks, name, i, h):
-            chunk, part = divmod(i, CHUNK_PASSES)
-            values = raw_chunks[chunk][:, 0, part * PASS_PIX : (part + 1) * PASS_PIX]
+        def load_pass(raw, dram_rows, name, i):
+            new_pass(raw, name, i)
+            load(raw[i], dram_rows, i)
+
+        def load_chunk(raw, dram_rows, name, chunk):
+            whole = rows.tile([P, ROW_TILES, CHUNK_PIX], BF16, name=name)
+            load(whole[:], dram_rows, chunk * CHUNK_PASSES)
+            for part in range(CHUNK_PASSES):
+                raw[chunk * CHUNK_PASSES + part] = whole[:, :, part * PASS_PIX : (part + 1) * PASS_PIX]
+
+        def ease_change(raw, name, i, h):
+            values = raw[i][:, 0, :]
             bank = turned.tile([P, 2, BANK_ROWS], F32, name="%s_bank%d" % (name, h))
             nc.tensor.matmul(bank[:, 0, :EASE_COLS], lhsT=values[:, :P], rhs=values[:, :EASE_COLS], start=True, stop=True)
             return bank
 
-        def turn(raw_chunks, name, i, h, bank=None):
-            chunk, part = divmod(i, CHUNK_PASSES)
-            words = raw_chunks[chunk][:].bitcast(F32)
+        def turn(raw, name, i, h, bank=None):
+            words = raw[i].bitcast(F32)
             if bank is None:
                 bank = turned.tile([P, 2, BANK_ROWS], F32, name="%s_bank%d" % (name, h))
             for u in range(2):
-                first = part * PASS_WORDS + u * P
                 for j in range(BANK_ROWS // P):
                     nc.tensor.transpose(
                         bank[:, u, j * P : (j + 1) * P],
-                        words[:, h * (BANK_ROWS // P) + j, first : first + P],
+                        words[:, h * (BANK_ROWS // P) + j, u * P : (u + 1) * P],
                         identity[:],
                     )
             return bank
 
-        def refill(raw_chunks, dram_rows, name, i):
+        def refill(raw, dram_rows, name, i):
             chunk, part = divmod(i, CHUNK_PASSES)
-            if part == CHUNK_PASSES - 1 and chunk + ROW_BUFS < N_CHUNK:
-                raw_chunks[chunk + ROW_BUFS] = load_chunk(dram_rows, name, chunk + ROW_BUFS)
+            if part == CHUNK_PASSES - 1 and FIRST_CHUNK <= chunk < N_CHUNK - ROW_BUFS:
+                load_chunk(raw, dram_rows, name, chunk + ROW_BUFS)
 
         def regroup_features(copy, grouped, bank, h):
             copy(
@@ -125,10 +124,9 @@ def tile_globalprototype_kernel(tc, features, prototypes, grad_out, out):
             )
 
         def inner_products(bank, i, t):
-            chunk, part = divmod(i, CHUNK_PASSES)
-            first = part * PASS_PIX + (t // 2) * 2 * P + t % 2
+            first = (t // 2) * 2 * P + t % 2
             for r in range(ROW_TILES):
-                pixels = f_raw[chunk][:, r, first : first + 2 * P - 1 : 2]
+                pixels = f_raw[i][:, r, first : first + 2 * P - 1 : 2]
                 nc.tensor.matmul(bank, lhsT=pixels, rhs=pixels, start=(r == 0), stop=(r == ROW_TILES - 1))
 
         def gram(i):
@@ -244,20 +242,19 @@ def tile_globalprototype_kernel(tc, features, prototypes, grad_out, out):
                     stop=(i == N_PASS - 1),
                 )
 
-        f_raw, g_raw = {}, {}
-        for chunk in range(2):
-            f_raw[chunk], g_raw[chunk] = new_chunk("f"), new_chunk("g")
-        load_pass(f_raw[0], f_rows, 0, slice(0, 2))
-        load_pass(f_raw[0], f_rows, 0, slice(2, 4))
-        load_pass(f_raw[0], f_rows, 1)
-        load_pass(g_raw[0], g_rows, 0)
-        load_pass(f_raw[1], f_rows, 2)
-        load_pass(g_raw[0], g_rows, 1)
-        load_pass(f_raw[1], f_rows, 3)
-        load(g_raw[1], g_rows, 1, slice(0, ROW_TILES), slice(0, CHUNK_PIX))
-        for chunk in range(2, ROW_BUFS):
-            f_raw[chunk] = load_chunk(f_rows, "f", chunk)
-            g_raw[chunk] = load_chunk(g_rows, "g", chunk)
+        new_pass(f_raw, "f", 0)
+        for half in (slice(0, 2), slice(2, 4)):
+            load(f_raw[0][:, half, :], f_rows, 0, half)
+        load_pass(f_raw, f_rows, "f", 1)
+        load_pass(g_raw, g_rows, "g", 0)
+        load_pass(f_raw, f_rows, "f", 2)
+        load_pass(g_raw, g_rows, "g", 1)
+        load_pass(f_raw, f_rows, "f", 3)
+        load_pass(g_raw, g_rows, "g", 2)
+        load_pass(g_raw, g_rows, "g", 3)
+        for chunk in range(FIRST_CHUNK, FIRST_CHUNK + ROW_BUFS):
+            load_chunk(f_raw, f_rows, "f", chunk)
+            load_chunk(g_raw, g_rows, "g", chunk)
         protos = const.tile([P, ROW_TILES, C], BF16, name="protos")
         nc.sync.dma_start(out=protos[:], in_=prototypes.rearrange("(r p) c -> p r c", p=P))
 
@@ -299,7 +296,6 @@ def tile_globalprototype_kernel(tc, features, prototypes, grad_out, out):
         sum_squares(f_grouped[0], sumsq[0], range(gram_places(0), PACK))
         turn_features(1, 0)
         turn_features(1, 1)
-        refill(f_raw, f_rows, "f", 1)
         head_gram(1)
         turn_gradients(0, 0)
         turn_gradients(0, 1)

@@ -1,7 +1,6 @@
 from contextlib import ExitStack
 
 import concourse.mybir as mybir
-from concourse.masks import make_identity
 
 F32 = mybir.dt.float32
 BF16 = mybir.dt.bfloat16
@@ -13,6 +12,7 @@ ACT = mybir.ActivationFunctionType
 ALU = mybir.AluOpType
 
 P = 128
+BLOCK = 32
 PACK = 4
 IMAGES, C, K, IMAGE_PIX = 4, 512, 512, 64 * 64
 ROW_TILES = 4
@@ -27,7 +27,7 @@ ROW_BUFS = 5
 BANK_ROWS = 2 * P
 
 
-SHARE_ROWS = 192
+SHARE_ROWS = (192, 144)
 EASE_COLS = 16
 WAIT_BANK = 2
 FIRST_DOUBLE = 9
@@ -65,7 +65,24 @@ def tile_globalprototype_kernel(tc, features, prototypes, grad_out, out):
         zeros = const.tile([P, P], F32, name="zeros")
         nc.vector.memset(zeros[:], 0.0)
         identity = const.tile([P, P], F32, name="identity")
-        make_identity(nc, identity[:])
+
+        def build_identity(identity):
+            ones = const.tile([P, BLOCK], F32, name="ones", align_bytes=64)
+            count = const.tile([P, BLOCK], F32, name="count", align_bytes=64)
+            turned_count = const.tile([P, BLOCK], F32, name="turned_count", align_bytes=64)
+            block = const.tile([P, BLOCK], F32, name="block")
+            nc.vector.memset(ones[:], 1.0)
+            nc.vector.tensor_tensor_scan(
+                out=count[:], data0=ones[:], data1=ones[:], initial=0.0, op0=ALU.mult, op1=ALU.add
+            )
+            nc.vector.memset(identity[:], 0.0)
+            nc.vector.transpose(out=turned_count[:], in_=count[:])
+            nc.vector.tensor_tensor(out=block[:], in0=count[:], in1=turned_count[:], op=ALU.is_equal)
+            for first in range(0, P, BLOCK):
+                part = slice(first, first + BLOCK)
+                nc.vector.tensor_copy(out=identity[part, part], in_=block[part, :])
+
+        build_identity(identity)
 
         m_sums = [sums.tile([P, C], F32, name="m_sum%d" % r) for r in range(ROW_TILES)]
 
@@ -189,23 +206,28 @@ def tile_globalprototype_kernel(tc, features, prototypes, grad_out, out):
             nc.vector.reciprocal(out=inv_norm[:], in_=norm[:])
             return inv_norm
 
-        def regroup_share(bank):
-            share = groups.tile([P, SHARE_ROWS, PACK], BF16, name="share", align_bytes=64)
+        def share_rows(i):
+            return SHARE_ROWS[i % 2]
+
+        def regroup_share(bank, i):
+            count = share_rows(i)
+            share = groups.tile([P, count, PACK], BF16, name="share", align_bytes=64)
             nc.scalar.copy(
-                out=share[:].bitcast(F32), in_=bank[:, :, BANK_ROWS - SHARE_ROWS :].rearrange("p u k -> p k u")
+                out=share[:].bitcast(F32), in_=bank[:, :, BANK_ROWS - count :].rearrange("p u k -> p k u")
             )
             return share
 
-        def scale_share(gs, share, inv_norm):
+        def scale_share(gs, share, inv_norm, i):
+            count = share_rows(i)
             nc.gpsimd.tensor_tensor(
-                out=gs[:, BANK_ROWS - SHARE_ROWS : BANK_ROWS, :],
+                out=gs[:, BANK_ROWS - count : BANK_ROWS, :],
                 in0=share[:],
-                in1=inv_norm[:].unsqueeze(1).to_broadcast([P, SHARE_ROWS, PACK]),
+                in1=inv_norm[:].unsqueeze(1).to_broadcast([P, count, PACK]),
                 op=ALU.mult,
             )
 
-        def scale_gradients(gs, bank, inv_norm, h):
-            count = BANK_ROWS - SHARE_ROWS if h == 0 else BANK_ROWS
+        def scale_gradients(gs, bank, inv_norm, h, i):
+            count = BANK_ROWS - share_rows(i) if h == 0 else BANK_ROWS
             per_pixel = inv_norm[:].rearrange("p (u e) -> p u e", u=2).unsqueeze(1)
             nc.vector.tensor_tensor(
                 out=gs[:, h * BANK_ROWS : h * BANK_ROWS + count, :].rearrange("p k (u e) -> p k u e", u=2),
@@ -306,7 +328,7 @@ def tile_globalprototype_kernel(tc, features, prototypes, grad_out, out):
         empty_features(1, 1, nc.scalar.copy)
         inv_norm[0] = inverse_norms(norm[0])
         head_diagonals(1)
-        share[0] = regroup_share(g_banks[0, 0])
+        share[0] = regroup_share(g_banks[0, 0], 0)
         sum_squares(f_grouped[1], sumsq[1], (2, 3))
         turn_features(2, 1)
         turn_features(2, 0)
@@ -315,14 +337,14 @@ def tile_globalprototype_kernel(tc, features, prototypes, grad_out, out):
         for i in range(N_PASS):
             gs[i] = groups.tile([P, K, PACK], BF16, name="gs", align_bytes=64)
             g_mx[i] = new_mx(K, "g")
-            scale_share(gs[i], share[i], inv_norm[i])
+            scale_share(gs[i], share[i], inv_norm[i], i)
             if 0 < i < last:
-                scale_gradients(gs[i], g_banks[i, 0], inv_norm[i], 0)
+                scale_gradients(gs[i], g_banks[i, 0], inv_norm[i], 0, i)
             if i == last:
                 quantise_features(i)
-            scale_gradients(gs[i], g_banks[i, 1], inv_norm[i], 1)
+            scale_gradients(gs[i], g_banks[i, 1], inv_norm[i], 1, i)
             if i == 0:
-                scale_gradients(gs[i], g_banks[i, 0], inv_norm[i], 0)
+                scale_gradients(gs[i], g_banks[i, 0], inv_norm[i], 0, i)
             if is_pass(i + 1):
                 sum_squares(f_grouped[i + 1], sumsq[i + 1], range(gram_places(i + 1), 2))
             if is_pass(i + 2):
@@ -346,7 +368,7 @@ def tile_globalprototype_kernel(tc, features, prototypes, grad_out, out):
             if i < last:
                 turn_gradients(i + 1, 1)
                 refill(g_raw, g_rows, "g", i + 1)
-                share[i + 1] = regroup_share(g_banks[i + 1, 0])
+                share[i + 1] = regroup_share(g_banks[i + 1, 0], i + 1)
             if i > 0:
                 multiply(i - 1, g_mx[i - 1], f_mx[i - 1], (0, 1))
             else:
@@ -412,7 +434,7 @@ def tile_globalprototype_kernel(tc, features, prototypes, grad_out, out):
 
         quantise(g_mx[last], gs[last], E5M2_X4, slice(BANK_ROWS, K))
         multiply(last, g_mx[last], f_mx[last], (2, 3))
-        scale_gradients(gs[last], g_banks[last, 0], inv_norm[last], 0)
+        scale_gradients(gs[last], g_banks[last, 0], inv_norm[last], 0, last)
         nc.vector.reciprocal(out=inv_p[:], in_=p_norm[:])
         nc.gpsimd.tensor_tensor(out=inv_p2[:], in0=inv_p[:], in1=inv_p[:], op=ALU.mult)
         nc.gpsimd.tensor_tensor(out=inv_p3[:], in0=inv_p2[:], in1=inv_p[:], op=ALU.mult)

from contextlib import ExitStack

import concourse.mybir as mybir

F32 = mybir.dt.float32
BF16 = mybir.dt.bfloat16
U32 = mybir.dt.uint32
U8 = mybir.dt.uint8
E4M3_X4 = mybir.dt.float8_e4m3fn_x4
E5M2_X4 = mybir.dt.float8_e5m2_x4
ACT = mybir.ActivationFunctionType
ALU = mybir.AluOpType

P = 128
BLOCK = 32
PACK = 4
IMAGES, C, K, IMAGE_PIX = 4, 512, 512, 64 * 64
ROW_TILES = 4
PASS_PIX = P * PACK
PASS_WORDS = PASS_PIX // 2
N_PASS = IMAGES * IMAGE_PIX // PASS_PIX
CHUNK_PASSES = 2
CHUNK_PIX = CHUNK_PASSES * PASS_PIX
N_CHUNK = N_PASS // CHUNK_PASSES
FIRST_CHUNK = 2
ROW_BUFS = 5
BANK_ROWS = 2 * P


SHARE_ROWS = (192, 144)
EASE_COLS = 16
WAIT_BANK = 2
FIRST_DOUBLE = 9


def gram_places(i):
    if i < 2:
        return 3 - i
    return 2 if i % 2 and i >= FIRST_DOUBLE else 1


FLOPS = 2 * K * C * IMAGES * IMAGE_PIX


def tile_globalprototype_kernel(tc, features, prototypes, grad_out, out):
    nc = tc.nc
    f_rows = features.rearrange("b (r p) h w -> b p r (h w)", p=P)
    g_rows = grad_out.rearrange("b (r p) h w -> b p r (h w)", p=P)
    out_rows = out.rearrange("(r p) c -> r p c", p=P)

    with ExitStack() as ctx:
        const = ctx.enter_context(tc.tile_pool(name="const", bufs=1))
        rows = ctx.enter_context(tc.tile_pool(name="rows", bufs=ROW_BUFS))
        groups = ctx.enter_context(tc.tile_pool(name="groups", bufs=5))
        packed = ctx.enter_context(tc.tile_pool(name="packed", bufs=6))
        small = ctx.enter_context(tc.tile_pool(name="small", bufs=4))
        scratch = ctx.enter_context(tc.tile_pool(name="scratch", bufs=4))
        turned = ctx.enter_context(tc.psum_pool(name="turned", bufs=1))
        sums = ctx.enter_context(tc.psum_pool(name="sums", bufs=1))
        ctx.enter_context(tc.manual_schedule())

        warm = const.tile([P, 1], F32, name="warm")
        nc.vector.memset(warm[:], 1.0)
        nc.scalar.activation(out=warm[:], in_=warm[:], func=ACT.Sqrt)
        zeros = const.tile([P, P], F32, name="zeros")
        nc.vector.memset(zeros[:], 0.0)
        identity = const.tile([P, P], F32, name="identity")

        def build_identity(identity):
            ones = const.tile([P, BLOCK], F32, name="ones", align_bytes=64)
            count = const.tile([P, BLOCK], F32, name="count", align_bytes=64)
            turned_count = const.tile([P, BLOCK], F32, name="turned_count", align_bytes=64)
            block = const.tile([P, BLOCK], F32, name="block")
            nc.vector.memset(ones[:], 1.0)
            nc.vector.tensor_tensor_scan(
                out=count[:], data0=ones[:], data1=ones[:], initial=0.0, op0=ALU.mult, op1=ALU.add
            )
            nc.vector.memset(identity[:], 0.0)
            nc.vector.transpose(out=turned_count[:], in_=count[:])
            nc.vector.tensor_tensor(out=block[:], in0=count[:], in1=turned_count[:], op=ALU.is_equal)
            for first in range(0, P, BLOCK):
                part = slice(first, first + BLOCK)
                nc.vector.tensor_copy(out=identity[part, part], in_=block[part, :])

        build_identity(identity)

        m_sums = [sums.tile([P, C], F32, name="m_sum%d" % r) for r in range(ROW_TILES)]

        def keep_clock(count):
            for n in range(count):
                nc.tensor.matmul(m_sums[WAIT_BANK][:, P : 2 * P], lhsT=zeros[:], rhs=zeros[:], start=True, stop=True)


        f_raw, g_raw = {}, {}

        def load(out, dram_rows, i, row_tiles=slice(0, ROW_TILES)):
            image, first = divmod(i * PASS_PIX, IMAGE_PIX)
            nc.sync.dma_start(out=out, in_=dram_rows[image, :, row_tiles, first : first + out.shape[2]])

        def new_pass(raw, name, i):
            raw[i] = rows.tile([P, ROW_TILES, PASS_PIX], BF16, name="%s_pass%d" % (name, i), bufs=1)[:]

        def load_pass(raw, dram_rows, name, i):
            new_pass(raw, name, i)
            load(raw[i], dram_rows, i)

        def load_chunk(raw, dram_rows, name, chunk):
            whole = rows.tile([P, ROW_TILES, CHUNK_PIX], BF16, name=name)
            load(whole[:], dram_rows, chunk * CHUNK_PASSES)
            for part in range(CHUNK_PASSES):
                raw[chunk * CHUNK_PASSES + part] = whole[:, :, part * PASS_PIX : (part + 1) * PASS_PIX]

        def ease_change(raw, name, i, h):
            values = raw[i][:, 0, :]
            bank = turned.tile([P, 2, BANK_ROWS], F32, name="%s_bank%d" % (name, h))
            nc.tensor.matmul(bank[:, 0, :EASE_COLS], lhsT=values[:, :P], rhs=values[:, :EASE_COLS], start=True, stop=True)
            return bank

        def turn(raw, name, i, h, bank=None):
            words = raw[i].bitcast(F32)
            if bank is None:
                bank = turned.tile([P, 2, BANK_ROWS], F32, name="%s_bank%d" % (name, h))
            for u in range(2):
                for j in range(BANK_ROWS // P):
                    nc.tensor.transpose(
                        bank[:, u, j * P : (j + 1) * P],
                        words[:, h * (BANK_ROWS // P) + j, u * P : (u + 1) * P],
                        identity[:],
                    )
            return bank

        def refill(raw, dram_rows, name, i):
            chunk, part = divmod(i, CHUNK_PASSES)
            if part == CHUNK_PASSES - 1 and FIRST_CHUNK <= chunk < N_CHUNK - ROW_BUFS:
                load_chunk(raw, dram_rows, name, chunk + ROW_BUFS)

        def regroup_features(copy, grouped, bank, h):
            copy(
                out=grouped[:].bitcast(F32)[:, h * BANK_ROWS : (h + 1) * BANK_ROWS, :],
                in_=bank[:].rearrange("p u c -> p c u"),
            )

        def inner_products(bank, i, t):
            first = (t // 2) * 2 * P + t % 2
            for r in range(ROW_TILES):
                pixels = f_raw[i][:, r, first : first + 2 * P - 1 : 2]
                nc.tensor.matmul(bank, lhsT=pixels, rhs=pixels, start=(r == 0), stop=(r == ROW_TILES - 1))

        def gram(i):
            bank = turned.tile([P, gram_places(i), P], F32, name="f_bank1")
            for t in range(gram_places(i)):
                inner_products(bank[:, t, :], i, t)
            return bank

        def take_diagonals(bank, i):
            for t in range(gram_places(i)):
                take_diagonal(bank[:, t, :], sumsq[i], t)

        def head_gram(i):
            for t in range(gram_places(i)):
                inner_products(m_sums[(3 * i + t) % ROW_TILES][:, :P], i, t)

        def head_diagonals(i):
            for t in range(gram_places(i)):
                take_diagonal(m_sums[(3 * i + t) % ROW_TILES][:, :P], sumsq[i], t)

        def take_diagonal(bank, sumsq, t=0):
            diagonal = scratch.tile([P, P], F32, name="diagonal")
            nc.vector.scalar_tensor_tensor(
                out=diagonal[:],
                in0=bank,
                scalar=1.0,
                in1=identity[:],
                op0=ALU.mult,
                op1=ALU.mult,
                accum_out=sumsq[:, t : t + 1],
            )

        def sum_squares(grouped, sumsq, slots):
            for t in slots:
                squares = scratch.tile([P, C], BF16, name="squares")
                nc.scalar.activation(
                    out=squares[:], in_=grouped[:, :, t], func=ACT.Square, accum_out=sumsq[:, t : t + 1]
                )

        def sum_squares_on_vector(grouped, sumsq, slots):
            for t in slots:
                squares = scratch.tile([P, C], BF16, name="squares_v")
                nc.vector.scalar_tensor_tensor(
                    out=squares[:],
                    in0=grouped[:, :, t],
                    scalar=1.0,
                    in1=grouped[:, :, t],
                    op0=ALU.mult,
                    op1=ALU.mult,
                    accum_out=sumsq[:, t : t + 1],
                )

        def roots(sumsq):
            norm = small.tile([P, PACK], F32, name="norm")
            nc.scalar.activation(out=norm[:], in_=sumsq[:], func=ACT.Sqrt)
            return norm

        def inverse_norms(norm):
            inv_norm = small.tile([P, PACK], F32, name="inv_norm")
            nc.vector.reciprocal(out=inv_norm[:], in_=norm[:])
            return inv_norm

        def share_rows(i):
            return SHARE_ROWS[i % 2]

        def regroup_share(bank, i):
            count = share_rows(i)
            share = groups.tile([P, count, PACK], BF16, name="share", align_bytes=64)
            nc.scalar.copy(
                out=share[:].bitcast(F32), in_=bank[:, :, BANK_ROWS - count :].rearrange("p u k -> p k u")
            )
            return share

        def scale_share(gs, share, inv_norm, i):
            count = share_rows(i)
            nc.gpsimd.tensor_tensor(
                out=gs[:, BANK_ROWS - count : BANK_ROWS, :],
                in0=share[:],
                in1=inv_norm[:].unsqueeze(1).to_broadcast([P, count, PACK]),
                op=ALU.mult,
            )

        def scale_gradients(gs, bank, inv_norm, h, i):
            count = BANK_ROWS - share_rows(i) if h == 0 else BANK_ROWS
            per_pixel = inv_norm[:].rearrange("p (u e) -> p u e", u=2).unsqueeze(1)
            nc.vector.tensor_tensor(
                out=gs[:, h * BANK_ROWS : h * BANK_ROWS + count, :].rearrange("p k (u e) -> p k u e", u=2),
                in0=bank[:].bitcast(BF16).rearrange("p u (k e) -> p k u e", e=2)[:, :count],
                in1=per_pixel.to_broadcast([P, count, 2, 2]),
                op=ALU.mult,
            )

        def new_mx(width, name):
            codes = packed.tile([P, width], U32, name=name + "_codes", align_bytes=64)
            scales = packed.tile([P, width], U8, name=name + "_scales", align_bytes=64)
            return codes, scales

        def quantise(mx, grouped, fmt, cols):
            codes, scales = mx
            nc.vector.quantize_mx(
                out=codes[:, cols].bitcast(fmt),
                scales=scales[:, cols],
                in_=grouped[:, cols, :].rearrange("p w t -> p (w t)"),
            )

        def multiply(i, g_mx, f_mx, row_tiles):
            g_codes, g_scales = g_mx
            f_codes, f_scales = f_mx
            for r in row_tiles:
                k_cols = slice(r * P, (r + 1) * P)
                nc.tensor.matmul_mx(
                    out=m_sums[r][:],
                    lhsT=g_codes[:, k_cols].bitcast(E5M2_X4),
                    lhsT_scale=g_scales[:, k_cols],
                    rhs=f_codes[:].bitcast(E4M3_X4),
                    rhs_scale=f_scales[:],
                    start=(i == 0),
                    stop=(i == N_PASS - 1),
                )

        new_pass(f_raw, "f", 0)
        for half in (slice(0, 2), slice(2, 4)):
            load(f_raw[0][:, half, :], f_rows, 0, half)
        load_pass(f_raw, f_rows, "f", 1)
        load_pass(g_raw, g_rows, "g", 0)
        load_pass(f_raw, f_rows, "f", 2)
        load_pass(g_raw, g_rows, "g", 1)
        load_pass(f_raw, f_rows, "f", 3)
        load_pass(g_raw, g_rows, "g", 2)
        load_pass(g_raw, g_rows, "g", 3)
        for chunk in range(FIRST_CHUNK, FIRST_CHUNK + ROW_BUFS):
            load_chunk(f_raw, f_rows, "f", chunk)
            load_chunk(g_raw, g_rows, "g", chunk)
        protos = const.tile([P, ROW_TILES, C], BF16, name="protos")
        nc.sync.dma_start(out=protos[:], in_=prototypes.rearrange("(r p) c -> p r c", p=P))

        def is_pass(j):
            return 0 <= j < N_PASS

        last = N_PASS - 1
        f_banks, g_banks, f_grouped, share, sumsq, norm, inv_norm, gs, f_mx, g_mx = [{} for n in range(10)]

        def turn_features(j, h, bank=None):
            f_banks[j, h] = turn(f_raw, "f", j, h, bank)

        def turn_gradients(j, h):
            g_banks[j, h] = turn(g_raw, "g", j, h)

        def empty_features(j, h, copy):
            regroup_features(copy, f_grouped[j], f_banks[j, h], h)

        def new_features(j):
            f_grouped[j] = groups.tile([P, C, PACK], BF16, name="f_grouped", align_bytes=64)
            sumsq[j] = small.tile([P, PACK], F32, name="sumsq")

        def take_roots(j):
            norm[j] = roots(sumsq[j])

        def quantise_features(j):
            f_mx[j] = new_mx(C, "f")
            quantise(f_mx[j], f_grouped[j], E4M3_X4, slice(0, C))

        keep_clock(4)
        turn_features(0, 0)
        turn_features(0, 1)
        new_features(0)
        new_features(1)
        empty_features(0, 0, nc.scalar.copy)
        empty_features(0, 1, nc.vector.tensor_copy)
        head_gram(0)
        head_diagonals(0)
        sum_squares(f_grouped[0], sumsq[0], range(gram_places(0), PACK))
        turn_features(1, 0)
        turn_features(1, 1)
        head_gram(1)
        turn_gradients(0, 0)
        turn_gradients(0, 1)
        keep_clock(2)
        quantise_features(0)
        empty_features(1, 0, nc.scalar.copy)
        take_roots(0)
        empty_features(1, 1, nc.scalar.copy)
        inv_norm[0] = inverse_norms(norm[0])
        head_diagonals(1)
        share[0] = regroup_share(g_banks[0, 0], 0)
        sum_squares(f_grouped[1], sumsq[1], (2, 3))
        turn_features(2, 1)
        turn_features(2, 0)
        keep_clock(2)

        for i in range(N_PASS):
            gs[i] = groups.tile([P, K, PACK], BF16, name="gs", align_bytes=64)
            g_mx[i] = new_mx(K, "g")
            scale_share(gs[i], share[i], inv_norm[i], i)
            if 0 < i < last:
                scale_gradients(gs[i], g_banks[i, 0], inv_norm[i], 0, i)
            if i == last:
                quantise_features(i)
            scale_gradients(gs[i], g_banks[i, 1], inv_norm[i], 1, i)
            if i == 0:
                scale_gradients(gs[i], g_banks[i, 0], inv_norm[i], 0, i)
            if is_pass(i + 1):
                sum_squares(f_grouped[i + 1], sumsq[i + 1], range(gram_places(i + 1), 2))
            if is_pass(i + 2):
                new_features(i + 2)
                empty_features(i + 2, 1, nc.scalar.copy)
            if i < last:
                take_roots(i + 1)
            if i + 1 < last:
                quantise_features(i + 1)
            if i < last:
                inv_norm[i + 1] = inverse_norms(norm[i + 1])
                turn_gradients(i + 1, 0)
            if is_pass(i + 2):
                empty_features(i + 2, 0, nc.scalar.copy)
            if i < last:
                quantise(g_mx[i], gs[i], E5M2_X4, slice(0, K))
            if i > 0:
                multiply(i - 1, g_mx[i - 1], f_mx[i - 1], (2, 3))
            if is_pass(i + 2):
                f_gram = gram(i + 2)
            if i < last:
                turn_gradients(i + 1, 1)
                refill(g_raw, g_rows, "g", i + 1)
                share[i + 1] = regroup_share(g_banks[i + 1, 0], i + 1)
            if i > 0:
                multiply(i - 1, g_mx[i - 1], f_mx[i - 1], (0, 1))
            else:
                keep_clock(3)
            if is_pass(i + 2):
                take_diagonals(f_gram, i + 2)
                sum_squares(f_grouped[i + 2], sumsq[i + 2], (2, 3))
            if is_pass(i + 3):
                turn_features(i + 3, 1, ease_change(f_raw, "f", i + 3, 1))
                turn_features(i + 3, 0)
                refill(f_raw, f_rows, "f", i + 3)

        p_sumsq = const.tile([P, ROW_TILES], F32, name="p_sumsq")
        p_squares = const.tile([P, ROW_TILES, C], BF16, name="p_squares")
        for r in range(ROW_TILES):
            nc.scalar.activation(
                out=p_squares[:, r, :], in_=protos[:, r, :], func=ACT.Square, accum_out=p_sumsq[:, r : r + 1]
            )
        p_norm = const.tile([P, ROW_TILES], F32, name="p_norm")
        nc.scalar.activation(out=p_norm[:], in_=p_sumsq[:], func=ACT.Sqrt)
        inv_p = const.tile([P, ROW_TILES], F32, name="inv_p")
        inv_p2 = const.tile([P, ROW_TILES], F32, name="inv_p2")
        inv_p3 = const.tile([P, ROW_TILES], F32, name="inv_p3")

        proj = const.tile([P, ROW_TILES], F32, name="proj")
        pull = const.tile([P, ROW_TILES], F32, name="pull")
        products = const.tile([P, ROW_TILES, C], F32, name="products")
        m_scaled = const.tile([P, ROW_TILES, C], F32, name="m_scaled")
        result = const.tile([P, ROW_TILES, C], F32, name="result")

        def project(r):
            nc.vector.scalar_tensor_tensor(
                out=products[:, r, :],
                in0=m_sums[r][:],
                scalar=1.0,
                in1=protos[:, r, :],
                op0=ALU.mult,
                op1=ALU.mult,
                accum_out=proj[:, r : r + 1],
            )
            nc.scalar.activation(out=m_scaled[:, r, :], in_=m_sums[r][:], func=ACT.Copy, scale=inv_p[:, r : r + 1])

        def pull_back(r):
            nc.vector.scalar_tensor_tensor(
                out=pull[:, r : r + 1],
                in0=proj[:, r : r + 1],
                scalar=-1.0,
                in1=inv_p3[:, r : r + 1],
                op0=ALU.mult,
                op1=ALU.mult,
            )

        def finish(r):
            nc.vector.scalar_tensor_tensor(
                out=result[:, r, :],
                in0=protos[:, r, :],
                scalar=pull[:, r : r + 1],
                in1=m_scaled[:, r, :],
                op0=ALU.mult,
                op1=ALU.add,
            )
            nc.sync.dma_start(out=out_rows[r], in_=result[:, r, :])

        quantise(g_mx[last], gs[last], E5M2_X4, slice(BANK_ROWS, K))
        multiply(last, g_mx[last], f_mx[last], (2, 3))
        scale_gradients(gs[last], g_banks[last, 0], inv_norm[last], 0, last)
        nc.vector.reciprocal(out=inv_p[:], in_=p_norm[:])
        nc.gpsimd.tensor_tensor(out=inv_p2[:], in0=inv_p[:], in1=inv_p[:], op=ALU.mult)
        nc.gpsimd.tensor_tensor(out=inv_p3[:], in0=inv_p2[:], in1=inv_p[:], op=ALU.mult)
        quantise(g_mx[last], gs[last], E5M2_X4, slice(0, BANK_ROWS))
        multiply(last, g_mx[last], f_mx[last], (0, 1))
        project(2)
        project(3)
        pull_back(2)
        project(0)
        pull_back(3)
        finish(2)
        project(1)
        pull_back(0)
        finish(3)
        pull_back(1)
        finish(0)
        finish(1)
